import numpy as np
import ml_dtypes


def mxq(x, axis, fmt="e4m3"):
    dtype, down = {"e4m3": (ml_dtypes.float8_e4m3fn, 7), "e5m2": (ml_dtypes.float8_e5m2, 14)}[fmt]
    v = np.moveaxis(np.asarray(x, np.float32).astype(ml_dtypes.bfloat16).astype(np.float64), axis, -1)
    blocks = v.reshape(v.shape[:-1] + (-1, 32))
    amax = np.abs(blocks).max(-1, keepdims=True)
    byte = np.maximum(np.where(amax > 0, np.frexp(amax)[1] - 1 + 127, 0) - down, 1)
    scale = np.exp2(byte - 127.0)
    codes = (blocks / scale).astype(np.float32).astype(dtype).astype(np.float64)
    return np.moveaxis((codes * scale).reshape(v.shape), -1, axis)


WIDE = False


def mx_kscale(k):
    if not WIDE:
        return np.ones(k)
    levels = np.array([10, -10, 5, -5, 0])
    if k % 512:
        return np.exp2(np.random.permutation(np.resize(levels, k // 32))).repeat(32)
    a = np.empty((k // 512, 16))
    for p in range(k // 512):
        a[p, :8] = np.random.permutation(np.resize(levels, 8))
        for g in range(8):
            far = levels[np.abs(levels - a[p, g]) >= 10]
            a[p, g + 8] = far[np.random.randint(len(far))]
    return np.exp2(a.ravel()).repeat(32)


BF16 = ml_dtypes.bfloat16


def bf(x):
    return np.asarray(x, np.float32).astype(BF16)


def f64(x):
    return np.asarray(x).astype(np.float64)


B, T, D, DH, H, W = 1, 8192, 512, 64, 4, 512
ROPE_BASE = 10000.0
EPS = 1.1920929e-07


def rope(u):
    freqs = ROPE_BASE ** (-2.0 * np.arange(DH // 2) / DH)
    theta = np.arange(T)[:, None] * freqs[None, :]
    cos, sin = np.cos(theta), np.sin(theta)
    u1, u2 = u[..., 0::2], u[..., 1::2]
    return np.stack([u1 * cos - u2 * sin, u1 * sin + u2 * cos], axis=-1).reshape(u.shape)


def rmsnorm(u, w):
    return u * (1.0 / np.sqrt(np.mean(u * u, axis=-1, keepdims=True) + EPS)) * w


def setup_inputs():
    s = mx_kscale(D)
    return {"x": bf(np.random.standard_normal((B, T, D)) * s),
            "wq": bf(np.random.standard_normal((H * DH, D)) / np.sqrt(D) / s),
            "wkv": bf(np.random.standard_normal((2 * DH, D)) * 2.0 / np.sqrt(D) / s),
            "q_norm_w": bf(1.0 + 0.1 * np.random.standard_normal(DH)),
            "k_norm_w": bf(1.0 + 0.1 * np.random.standard_normal(DH))}


def reference(x, wq, wkv, q_norm_w, k_norm_w):
    xq = mxq(f64(x), 2, "e4m3")
    q = xq @ mxq(f64(wq), 1, "e4m3").T
    kv = xq @ mxq(f64(wkv), 1, "e4m3").T
    k, v = kv[..., :DH], kv[..., DH:]
    q = q.reshape(B, T, H, DH).transpose(0, 2, 1, 3)
    q_rot = rmsnorm(rope(q), f64(q_norm_w))
    k_rot = rmsnorm(rope(k), f64(k_norm_w))
    return q_rot, k_rot, v

@@ -1,0 +1,379 @@
+from contextlib import ExitStack
+
+import concourse.mybir as mybir
+from concourse.masks import make_identity
+
+FLOPS = 2 * 8192 * 512 * 384
+
+F32 = mybir.dt.float32
+BF16 = mybir.dt.bfloat16
+I32 = mybir.dt.int32
+U32 = mybir.dt.uint32
+U8 = mybir.dt.uint8
+FP8X4 = mybir.dt.float8_e4m3fn_x4
+ALU = mybir.AluOpType
+ACT = mybir.ActivationFunctionType
+
+P = 128
+D = 512
+DH = 64
+NPAIR = 32
+NT = 64
+CH = 8
+NCH = 8
+GR = 4
+NGR = 16
+SL = 4
+D1 = 2
+D2 = 3
+EPS = 1.1920929e-07
+TWO_PI = 6.283185307179586
+WCOLS = 704
+
+
+def turn_constants():
+    his = []
+    los = []
+    for i in range(NPAIR):
+        f = 10000.0 ** (-2.0 * i / DH) / TWO_PI
+        e = 0
+        while f * 2.0 ** e < 1.0:
+            e += 1
+        scale = 2.0 ** (e + 13)
+        hi = int(f * scale) / scale
+        his.append(hi)
+        los.append(f - hi)
+    return his, los
+
+
+def tile_attention_pa_t_kernel(tc, x, wq, wkv, q_norm_w, k_norm_w, out_0, out_1, out_2):
+    nc = tc.nc
+    with ExitStack() as ctx:
+        ctx.enter_context(tc.manual_schedule())
+        consts = ctx.enter_context(tc.tile_pool(name="consts", bufs=1))
+        xin = ctx.enter_context(tc.tile_pool(name="xin", bufs=3))
+        grps = ctx.enter_context(tc.tile_pool(name="grps", bufs=6))
+        small = ctx.enter_context(tc.tile_pool(name="small", bufs=4))
+        junks = ctx.enter_context(tc.tile_pool(name="junks", bufs=8))
+        psum = ctx.enter_context(tc.psum_pool(name="psum", bufs=1))
+
+        xv = x[0].rearrange("(p j) k -> p j k", j=NT)
+        oqv = out_0[0].rearrange("h (p j) d -> p h j d", j=NT)
+        okv = out_1[0].rearrange("(p j) d -> p j d", j=NT)
+        ovv = out_2[0].rearrange("(p j) d -> p j d", j=NT)
+
+        ident = consts.tile([P, P], F32, name="ident")
+        perm = consts.tile([P, P], F32, name="perm")
+        ones = consts.tile([P, 1], F32, name="ones")
+        eps_t = consts.tile([P, 1], F32, name="eps_t")
+        gq_bf = consts.tile([P, DH], BF16, name="gq_bf")
+        gk_bf = consts.tile([P, DH], BF16, name="gk_bf")
+        gq = consts.tile([P, DH], F32, name="gq")
+        gk = consts.tile([P, DH], F32, name="gk")
+        wc = consts.tile([P, WCOLS], U32, name="wc", align_bytes=64)
+        ws = consts.tile([P, WCOLS], U8, name="ws", align_bytes=64)
+        xc = consts.tile([P, NT * P], U32, name="xc", align_bytes=64)
+        xs = consts.tile([P, NT * P], U8, name="xs", align_bytes=64)
+        base = consts.tile([P, NT, 2 * NPAIR], F32, name="base")
+        qtab = consts.tile([P, NT, 2 * DH], F32, name="qtab")
+
+        x32 = {}
+        grp = {}
+
+        def bank(n, shape):
+            return psum.tile(shape, F32, name="b%d" % n)
+
+        def ev_bank(e):
+            c, b = divmod(e, 4)
+            if b == 0:
+                grp[c] = grps.tile([P, 4096], BF16, name="grp", align_bytes=64)
+            xt = bank(e % 4, [P, 4, P])
+            for a in range(2):
+                for u in range(2):
+                    nc.tensor.transpose(xt[:, 2 * a + u, :], x32[c][:, 2 * b + a, u:2 * P:2], ident[:])
+            grf = grp[c][:].bitcast(F32).rearrange("p (b a r u) -> p b a r u", b=4, a=2, u=2)
+            nc.scalar.copy(out=grf[:, b], in_=xt[:].rearrange("p (a u) r -> p a r u", u=2))
+
+        def qx(c):
+            cols = slice(c * CH * P, (c + 1) * CH * P)
+            nc.vector.quantize_mx(out=xc[:, cols].bitcast(FP8X4), scales=xs[:, cols], in_=grp[c][:])
+
+        def qgh(h):
+            js = slice(GR * h, GR * h + GR)
+            nc.vector.tensor_tensor(
+                out=qtab[:, js, :].rearrange("p j (c i e) -> p (j c) i e", c=2, e=2),
+                in0=base[:, js, :].rearrange("p j (c i) -> p (j c) i", c=2).unsqueeze(3).to_broadcast(
+                    [P, 2 * GR, NPAIR, 2]),
+                in1=gq[:].rearrange("p (i e) -> p i e", e=2).unsqueeze(1).to_broadcast([P, 2 * GR, NPAIR, 2]),
+                op=ALU.mult)
+
+        with tc.tile_pool(name="pro", bufs=1) as pro, tc.tile_pool(name="tabs", bufs=4) as tabs:
+            w_sb = pro.tile([P, 3, D], BF16, name="w_sb")
+            nc.scalar.dma_start(out=w_sb[:, 0:2, :], in_=wq.rearrange("(r p) k -> p r k", p=P))
+            nc.scalar.dma_start(out=w_sb[:, 2, :], in_=wkv)
+            nc.scalar.dma_start(out=gq_bf[:], in_=q_norm_w.partition_broadcast(P))
+            nc.scalar.dma_start(out=gk_bf[:], in_=k_norm_w.partition_broadcast(P))
+            for c in range(NCH):
+                x_sb = xin.tile([P, CH, D], BF16, name="x_sb")
+                nc.sync.dma_start(out=x_sb[:], in_=xv[:, c * CH:(c + 1) * CH, :])
+                x32[c] = x_sb[:].bitcast(F32)
+
+            make_identity(nc, ident[:])
+            t1i = pro.tile([P, NCH], I32, name="t1i")
+            nc.gpsimd.iota(t1i[:], pattern=[[CH, NCH]], base=0, channel_multiplier=NT)
+            j0i = pro.tile([P, CH], I32, name="j0i")
+            nc.gpsimd.iota(j0i[:], pattern=[[1, CH]], base=0, channel_multiplier=0)
+            nc.vector.memset(ones[:], 1.0)
+            nc.vector.memset(eps_t[:], EPS)
+            his, los = turn_constants()
+            fhi = pro.tile([P, NPAIR], F32, name="fhi")
+            flo = pro.tile([P, NPAIR], F32, name="flo")
+            for i in range(NPAIR):
+                nc.vector.memset(fhi[:, i:i + 1], his[i])
+                nc.scalar.activation(out=flo[:, i:i + 1], in_=ones[:], func=ACT.Copy, scale=los[i])
+            idv = ident[:].rearrange("p (i e) -> p e i", e=2)
+            pmv = perm[:].rearrange("p (i e) -> p e i", e=2)
+            nc.vector.tensor_copy(out=pmv[:, 0], in_=idv[:, 1])
+            nc.vector.tensor_copy(out=pmv[:, 1], in_=idv[:, 0])
+            t1f = pro.tile([P, NCH], F32, name="t1f")
+            j0f = pro.tile([P, CH], F32, name="j0f")
+            nc.vector.tensor_copy(out=t1f[:], in_=t1i[:])
+            nc.vector.tensor_copy(out=j0f[:], in_=j0i[:])
+
+            w32 = w_sb[:].bitcast(F32)
+            gw = pro.tile([P, WCOLS * 4], BF16, name="gw", align_bytes=64)
+            gwf = gw[:].bitcast(F32).rearrange("p (c u) -> p c u", u=2)
+            gwb = gw[:].rearrange("p (i e u f) -> p e i u f", e=2, u=2, f=2)
+
+            def w_transposes(dst, slot, r, mat):
+                for u in range(2):
+                    nc.tensor.transpose(dst[:, slot + u, :], w32[:, r, u:2 * P:2], mat[:])
+
+            def plain_cols(src, slot, cb):
+                nc.scalar.copy(out=gwf[:, cb:cb + P, :], in_=src[:, slot:slot + 2, :].rearrange("p u c -> p c u"))
+
+            def swapped_cols(src, slot, cb, n):
+                sv = src[:, slot:slot + 2, 0:n].rearrange("p u (i e) -> p e i u", e=2)
+                dv = gwf[:, cb:cb + n, :].rearrange("p (i e) u -> p e i u", e=2)
+                nc.vector.tensor_copy(out=dv[:, 1], in_=sv[:, 1])
+                sb = src[:].bitcast(BF16)[:, slot:slot + 2, 0:2 * n].rearrange("p u (i e f) -> p e i u f", e=2, f=2)
+                nc.vector.tensor_scalar(out=gwb[:, 0, cb // 2:(cb + n) // 2], in0=sb[:, 0], scalar1=-1.0,
+                                        scalar2=None, op0=ALU.mult)
+
+            pa = bank(4, [P, 4, P])
+            w_transposes(pa, 0, 0, ident)
+            w_transposes(pa, 2, 1, ident)
+            pb = bank(5, [P, 4, P])
+            w_transposes(pb, 0, 2, ident)
+            w_transposes(pb, 2, 2, perm)
+            pc = bank(6, [P, 4, P])
+            w_transposes(pc, 0, 0, perm)
+            w_transposes(pc, 2, 1, perm)
+            plain_cols(pa, 0, 256)
+            plain_cols(pa, 2, 384)
+            plain_cols(pb, 0, 576)
+
+            def outer(dst, col, row):
+                nc.vector.tensor_tensor(out=dst[:], in0=col[:].unsqueeze(2).to_broadcast([P, 8, NPAIR]),
+                                        in1=row[:].unsqueeze(1).to_broadcast([P, 8, NPAIR]), op=ALU.mult)
+
+            def flat(t):
+                return t[:].rearrange("p a i -> p (a i)")
+
+            uh = pro.tile([P, 8, NPAIR], F32, name="uh")
+            ki = pro.tile([P, 8, NPAIR], I32, name="ki")
+            kf = pro.tile([P, 8, NPAIR], F32, name="kf")
+            ul = pro.tile([P, 8, NPAIR], F32, name="ul")
+            na = pro.tile([P, 8, NPAIR], F32, name="na")
+            bh = pro.tile([P, 8, NPAIR], F32, name="bh")
+            bl = pro.tile([P, 8, NPAIR], F32, name="bl")
+            bb = pro.tile([P, 8, 2, NPAIR], F32, name="bb")
+            nb = pro.tile([P, 16, NPAIR], F32, name="nb")
+            bbf = bb[:].rearrange("p a c i -> p (a c i)")
+            outer(uh, t1f, fhi)
+            outer(bh, j0f, fhi)
+            nc.vector.tensor_copy(out=ki[:], in_=uh[:])
+            outer(bl, j0f, flo)
+            nc.vector.tensor_copy(out=kf[:], in_=ki[:])
+            outer(ul, t1f, flo)
+            nc.vector.tensor_tensor(out=uh[:], in0=uh[:], in1=kf[:], op=ALU.subtract)
+            nc.vector.tensor_tensor(out=bb[:, :, 0, :], in0=bh[:], in1=bl[:], op=ALU.add)
+            nc.vector.tensor_tensor(out=uh[:], in0=uh[:], in1=ul[:], op=ALU.add)
+            nc.vector.tensor_scalar(out=bb[:, :, 1, :], in0=bb[:, :, 0, :], scalar1=0.25, scalar2=None, op0=ALU.add)
+            nc.vector.scalar_tensor_tensor(out=flat(na), in0=flat(uh), scalar=0.5, in1=flat(uh), op0=ALU.is_ge,
+                                           op1=ALU.subtract)
+            nc.vector.scalar_tensor_tensor(out=flat(nb), in0=bbf, scalar=1.0, in1=bbf, op0=ALU.is_ge,
+                                           op1=ALU.subtract)
+
+            swapped_cols(pb, 2, 512, DH)
+            swapped_cols(pc, 0, 0, P)
+            swapped_cols(pc, 2, 128, P)
+
+            for e in range(9):
+                ev_bank(e)
+
+            for c in range(NCH):
+                nv = tabs.tile([P, 16, NPAIR], F32, name="nv")
+                nc.gpsimd.tensor_tensor(out=nv[:], in0=nb[:],
+                                        in1=na[:, c, :].unsqueeze(1).to_broadcast([P, 16, NPAIR]), op=ALU.add)
+                if c >= 2:
+                    qgh(c - 2)
+                nc.vector.scalar_tensor_tensor(out=flat(nv), in0=flat(nv), scalar=-0.5, in1=flat(nv), op0=ALU.is_lt,
+                                               op1=ALU.add)
+                if c == 0:
+                    nc.vector.quantize_mx(out=wc[:, 0:512].bitcast(FP8X4), scales=ws[:, 0:512], in_=gw[:, 0:2048])
+                    nc.vector.quantize_mx(out=wc[:, 512:640].bitcast(FP8X4), scales=ws[:, 512:640],
+                                          in_=gw[:, 2048:2560])
+                    nc.vector.quantize_mx(out=wc[:, 640:704].bitcast(FP8X4), scales=ws[:, 640:704],
+                                          in_=gw[:, 2560:2816])
+                    nc.vector.tensor_copy(out=gq[:], in_=gq_bf[:])
+                    nc.vector.tensor_copy(out=gk[:], in_=gk_bf[:])
+                nc.scalar.activation(out=base[:, c * CH:(c + 1) * CH, :].rearrange("p j m -> p (j m)"), in_=flat(nv),
+                                     func=ACT.Sin, scale=-TWO_PI)
+                ev_bank(9 + c)
+
+        for e in range(17, 32):
+            ev_bank(e)
+        for c in range(NCH):
+            qx(c)
+
+        work = ctx.enter_context(tc.tile_pool(name="work", bufs=2))
+        outs = ctx.enter_context(tc.tile_pool(name="outs", bufs=2))
+
+        ps_t = {}
+        ss_t = {}
+        rs_t = {}
+        ov_t = {}
+        oq_t = {}
+        ok_t = {}
+        tq_t = {}
+        tk_t = {}
+        pq_t = {}
+        pk_t = {}
+
+        def lhs_of(j):
+            return xc[:, j * P:(j + 1) * P].bitcast(FP8X4), xs[:, j * P:(j + 1) * P]
+
+        def m1(j):
+            ps = bank(4 + j % 3, [P, 384])
+            ps_t[j] = ps
+            lhs, lsc = lhs_of(j)
+            nc.tensor.matmul_mx(out=ps[:, 0:256], lhsT=lhs, lhsT_scale=lsc, rhs=wc[:, 256:512].bitcast(FP8X4),
+                                rhs_scale=ws[:, 256:512], start=True, stop=True)
+            nc.tensor.matmul_mx(out=ps[:, 256:384], lhsT=lhs, lhsT_scale=lsc, rhs=wc[:, 576:704].bitcast(FP8X4),
+                                rhs_scale=ws[:, 576:704], start=True, stop=True)
+
+        def squares(j):
+            q, i = divmod(j, GR)
+            c, jj = divmod(j, CH)
+            if i == 0:
+                ss_t[q] = small.tile([P, 5 * GR], F32, name="ss")
+            if jj == 0:
+                ov_t[c] = outs.tile([P, CH, DH], F32, name="ov", bufs=3)
+            ps = ps_t[j]
+            junk = junks.tile([P, 5, DH], BF16, name="junk")
+            for h in range(5):
+                nc.scalar.activation(out=junk[:, h, :], in_=ps[:, h * DH:(h + 1) * DH], func=ACT.Square,
+                                     accum_out=ss_t[q][:, i * 5 + h:i * 5 + h + 1])
+            nc.scalar.copy(out=ov_t[c][:, jj, :], in_=ps[:, 320:384])
+            if i == GR - 1:
+                rs_t[q] = small.tile([P, 5 * GR], F32, name="rs")
+                nc.scalar.activation(out=rs_t[q][:], in_=ss_t[q][:], func=ACT.Abs_reciprocal_sqrt, scale=1.0 / DH,
+                                     bias=eps_t[:])
+
+        def m2q(j):
+            pq = bank(j % 4, [P, 512])
+            pq_t[j] = pq
+            lhs, lsc = lhs_of(j)
+            nc.tensor.matmul_mx(out=pq[:], lhsT=lhs, lhsT_scale=lsc, rhs=wc[:, 0:512].bitcast(FP8X4),
+                                rhs_scale=ws[:, 0:512], start=True, stop=True)
+
+        def m2k(q):
+            pk = bank(7, [P, GR, 2 * DH])
+            pk_t[q] = pk
+            for i in range(GR):
+                lhs, lsc = lhs_of(q * GR + i)
+                nc.tensor.matmul_mx(out=pk[:, i, :], lhsT=lhs, lhsT_scale=lsc, rhs=wc[:, 512:640].bitcast(FP8X4),
+                                    rhs_scale=ws[:, 512:640], start=True, stop=True)
+
+        def rope(j):
+            q, i = divmod(j, GR)
+            c, jj = divmod(j, CH)
+            if i == 0:
+                tq_t[q] = work.tile([P, GR, 512], F32, name="tq", bufs=3)
+            if jj == 0:
+                tk_t[c] = work.tile([P, CH, 2 * DH], F32, name="tk")
+            rs = rs_t[q]
+            pv = pq_t[j][:].rearrange("p (c h d) -> p h c d", c=2, h=4)
+            tv = tq_t[q][:, i, :].rearrange("p (c h d) -> p h c d", c=2, h=4)
+            for h in range(4):
+                nc.vector.scalar_tensor_tensor(out=tv[:, h], in0=pv[:, h], scalar=rs[:, i * 5 + h:i * 5 + h + 1],
+                                               in1=qtab[:, j, :].rearrange("p (c d) -> p c d", c=2), op0=ALU.mult,
+                                               op1=ALU.mult)
+            nc.vector.scalar_tensor_tensor(
+                out=tk_t[c][:, jj, :].rearrange("p (m e) -> p m e", e=2),
+                in0=pk_t[q][:, i, :].rearrange("p (m e) -> p m e", e=2), scalar=rs[:, i * 5 + 4:i * 5 + 5],
+                in1=base[:, j, :].unsqueeze(2).to_broadcast([P, 2 * NPAIR, 2]), op0=ALU.mult, op1=ALU.mult)
+
+        def add_q(eng, q, lo, hi):
+            c, half = divmod(q, 2)
+            if half == 0 and lo == 0:
+                oq_t[c] = outs.tile([P, 4, CH, DH], F32, name="oq")
+            tq = tq_t[q]
+            eng.tensor_tensor(
+                out=oq_t[c][:, :, half * GR + lo:half * GR + hi, :].rearrange("p h j d -> p j h d"),
+                in0=tq[:, lo:hi, 0:256].rearrange("p j (h d) -> p j h d", h=4),
+                in1=tq[:, lo:hi, 256:512].rearrange("p j (h d) -> p j h d", h=4), op=ALU.add)
+
+        def add_k(c, lo, hi):
+            if lo == 0:
+                ok_t[c] = outs.tile([P, CH, DH], F32, name="ok")
+            uk = work.tile([P, CH, DH], F32, name="uk")
+            nc.gpsimd.tensor_tensor(out=uk[:, lo:hi, :], in0=tk_t[c][:, lo:hi, 0:DH], in1=tk_t[c][:, lo:hi, DH:2 * DH],
+                                    op=ALU.add)
+            nc.gpsimd.tensor_tensor(out=ok_t[c][:, lo:hi, :], in0=uk[:, lo:hi, :],
+                                    in1=gk[:].unsqueeze(1).to_broadcast([P, hi - lo, DH]), op=ALU.mult)
+
+        def store(c, lo, hi):
+            js = slice(c * CH + lo, c * CH + hi)
+            nc.sync.dma_start(out=oqv[:, :, js, :], in_=oq_t[c][:, :, lo:hi, :])
+            nc.sync.dma_start(out=okv[:, js, :], in_=ok_t[c][:, lo:hi, :])
+
+        for a in range(D1):
+            m1(a)
+        for a in range(SL):
+            m1(a + D1)
+            squares(a)
+        for j in range(D2):
+            m2q(j)
+        m2k(0)
+
+        for q in range(NGR):
+            if 6 + q < NGR:
+                qgh(6 + q)
+            for i in range(GR):
+                j = q * GR + i
+                a = j + SL
+                if a + D1 < NT:
+                    m1(a + D1)
+                if i == 0 and q > 0:
+                    m2k(q)
+                if j + D2 < NT:
+                    m2q(j + D2)
+                if a < NT:
+                    squares(a)
+                    if a % CH == CH - 1:
+                        nc.sync.dma_start(out=ovv[:, a - CH + 1:a + 1, :], in_=ov_t[a // CH][:])
+                rope(j)
+            c = q // 2
+            add_q(nc.vector if (q % 4 == 3 or q >= NGR - 2) else nc.gpsimd, q, 0, GR)
+            if q < NGR - 2:
+                if q % 2 == 1:
+                    add_k(c, 0, CH)
+                    store(c, 0, CH)
+            elif q == NGR - 2:
+                add_k(c, 0, GR)
+                store(c, 0, GR)
+            else:
+                add_k(c, GR, CH)
+                store(c, GR, CH)

@@ -13,6 +13,7 @@ U8 = mybir.dt.uint8
 FP8X4 = mybir.dt.float8_e4m3fn_x4
 ALU = mybir.AluOpType
 ACT = mybir.ActivationFunctionType
+AX = mybir.AxisListType
 
 P = 128
 D = 512
@@ -22,13 +23,13 @@ NT = 64
 CH = 8
 NCH = 8
 GR = 4
-NGR = 16
-SL = 4
+NG = 16
 D1 = 2
 D2 = 3
 EPS = 1.1920929e-07
 TWO_PI = 6.283185307179586
 WCOLS = 704
+VECTOR_ADDS = (NG - 1,)
 
 
 def turn_constants():
@@ -51,10 +52,14 @@ def tile_attention_pa_t_kernel(tc, x, wq, wkv, q_norm_w, k_norm_w, out_0, out_1,
     with ExitStack() as ctx:
         ctx.enter_context(tc.manual_schedule())
         consts = ctx.enter_context(tc.tile_pool(name="consts", bufs=1))
-        xin = ctx.enter_context(tc.tile_pool(name="xin", bufs=3))
-        grps = ctx.enter_context(tc.tile_pool(name="grps", bufs=6))
+        xin = ctx.enter_context(tc.tile_pool(name="xin", bufs=NG))
+        grps = ctx.enter_context(tc.tile_pool(name="grps", bufs=3))
+        codes = ctx.enter_context(tc.tile_pool(name="codes", bufs=4))
         small = ctx.enter_context(tc.tile_pool(name="small", bufs=4))
         junks = ctx.enter_context(tc.tile_pool(name="junks", bufs=8))
+        tabs = ctx.enter_context(tc.tile_pool(name="tabs", bufs=3))
+        work = ctx.enter_context(tc.tile_pool(name="work", bufs=3))
+        outs = ctx.enter_context(tc.tile_pool(name="outs", bufs=3))
         psum = ctx.enter_context(tc.psum_pool(name="psum", bufs=1))
 
         xv = x[0].rearrange("(p j) k -> p j k", j=NT)
@@ -62,184 +67,119 @@ def tile_attention_pa_t_kernel(tc, x, wq, wkv, q_norm_w, k_norm_w, out_0, out_1,
         okv = out_1[0].rearrange("(p j) d -> p j d", j=NT)
         ovv = out_2[0].rearrange("(p j) d -> p j d", j=NT)
 
+        def bank(tag, shape):
+            return psum.tile(shape, F32, name=tag)
+
+        w_sb = consts.tile([P, 3, D], BF16, name="w_sb")
+        gains = consts.tile([P, 2 * DH], BF16, name="gains")
+        nc.gpsimd.memset(gains[:], 0.0)
+        nc.scalar.dma_start(out=w_sb[:, 0:2, :], in_=wq.rearrange("(r p) k -> p r k", p=P))
+        nc.scalar.dma_start(out=w_sb[:, 2, :], in_=wkv)
+        nc.scalar.dma_start(out=gains[0:1, 0:DH], in_=q_norm_w.unsqueeze(0))
+        nc.scalar.dma_start(out=gains[0:1, DH:2 * DH], in_=k_norm_w.unsqueeze(0))
+        x32 = {}
+        for g in range(NG):
+            x_sb = xin.tile([P, GR, D], BF16, name="x_sb")
+            nc.sync.dma_start(out=x_sb[:], in_=xv[:, g * GR:(g + 1) * GR, :])
+            x32[g] = x_sb[:].bitcast(F32)
+
         ident = consts.tile([P, P], F32, name="ident")
-        perm = consts.tile([P, P], F32, name="perm")
+        make_identity(nc, ident[:])
+        kpi = consts.tile([P, 1], I32, name="kpi")
+        nc.gpsimd.iota(kpi[:], pattern=[[0, 1]], base=0, channel_multiplier=1)
+        NPOS = P + 3 * CH
+        posi = consts.tile([P, NPOS], I32, name="posi")
+        nc.gpsimd.iota(posi[:, 0:P], pattern=[[NT, P]], base=0, channel_multiplier=0)
+        nc.gpsimd.iota(posi[:, P:P + 2 * CH], pattern=[[1, CH], [0, 2]], base=0, channel_multiplier=0)
+        nc.gpsimd.iota(posi[:, P + 2 * CH:NPOS], pattern=[[CH, CH]], base=0, channel_multiplier=0)
         ones = consts.tile([P, 1], F32, name="ones")
         eps_t = consts.tile([P, 1], F32, name="eps_t")
-        gq_bf = consts.tile([P, DH], BF16, name="gq_bf")
-        gk_bf = consts.tile([P, DH], BF16, name="gk_bf")
-        gq = consts.tile([P, DH], F32, name="gq")
-        gk = consts.tile([P, DH], F32, name="gk")
+        ones_bf = consts.tile([P, P], BF16, name="ones_bf")
+        nc.vector.memset(ones[:], 1.0)
+        nc.vector.memset(eps_t[:], EPS)
+        nc.vector.memset(ones_bf[:], 1.0)
+        warm = consts.tile([P, 2], F32, name="warm")
+        nc.scalar.activation(out=warm[:, 0:1], in_=ones[:], func=ACT.Sin)
+        his, los = turn_constants()
+        frow = consts.tile([P, 2, NPAIR], F32, name="frow")
+        for i in range(NPAIR):
+            nc.vector.memset(frow[:, 0, i:i + 1], his[i])
+            nc.scalar.activation(out=frow[:, 1, i:i + 1], in_=ones[:], func=ACT.Copy, scale=los[i])
+
+        kpf = consts.tile([P, 1], F32, name="kpf")
+        s4 = consts.tile([P, 1], F32, name="s4")
+        php = consts.tile([P, 1], F32, name="php")
+        phr = consts.tile([P, 1], F32, name="phr")
+        posf = consts.tile([P, NPOS], F32, name="posf")
+        mask = consts.tile([P, NPAIR], F32, name="mask")
+        fsel = consts.tile([P, 2, NPAIR], F32, name="fsel")
+        fk = consts.tile([P, 2], F32, name="fk")
+        un = consts.tile([P, NPOS], F32, name="un")
+        ki = consts.tile([P, NPOS], I32, name="ki")
+        kf = consts.tile([P, NPOS], F32, name="kf")
+        na = consts.tile([P, P + 2 * CH], F32, name="na")
+        nb = consts.tile([P, CH], F32, name="nb")
+        nb1 = consts.tile([P, CH], F32, name="nb1")
+        vr = consts.tile([P, 2 * CH], F32, name="vr")
+        brow = consts.tile([P, CH * 2 * NPAIR], F32, name="brow")
+        RC = slice(P, P + 2 * CH)
+        CC = slice(P + 2 * CH, NPOS)
+        nc.vector.tensor_copy(out=kpf[:], in_=kpi[:])
+        nc.vector.tensor_copy(out=posf[:], in_=posi[:])
+        nc.vector.tensor_scalar(out=s4[:], in0=kpf[:], scalar1=float(NPAIR), scalar2=0.25, op0=ALU.is_ge, op1=ALU.mult)
+        nc.vector.tensor_tensor(out=mask[:], in0=ident[:, 0:NPAIR], in1=ident[:, NPAIR:2 * NPAIR], op=ALU.add)
+        nc.vector.tensor_scalar(out=php[:], in0=s4[:], scalar1=-1.0, scalar2=0.25, op0=ALU.mult, op1=ALU.add)
+        nc.vector.tensor_scalar(out=phr[:], in0=s4[:], scalar1=0.25, scalar2=None, op0=ALU.add)
+        nc.vector.tensor_tensor(out=fsel[:], in0=frow[:], in1=mask[:].unsqueeze(1).to_broadcast([P, 2, NPAIR]),
+                                op=ALU.mult)
+        nc.vector.tensor_reduce(out=fk[:], in_=fsel[:], op=ALU.add, axis=AX.X)
+        nc.vector.tensor_scalar(out=un[:, 0:P], in0=posf[:, 0:P], scalar1=fk[:, 0:1], scalar2=php[:], op0=ALU.mult,
+                                op1=ALU.add)
+        unr = un[:, RC].rearrange("p (r c) -> p c r", c=2)
+        por = posf[:, RC].rearrange("p (r c) -> p c r", c=2)
+        nc.vector.tensor_scalar(out=unr[:, 0], in0=por[:, 0], scalar1=fk[:, 0:1], scalar2=s4[:], op0=ALU.mult,
+                                op1=ALU.add)
+        nc.vector.tensor_scalar(out=unr[:, 1], in0=por[:, 1], scalar1=fk[:, 0:1], scalar2=phr[:], op0=ALU.mult,
+                                op1=ALU.add)
+        nc.vector.tensor_scalar(out=un[:, CC], in0=posf[:, CC], scalar1=fk[:, 0:1], scalar2=None, op0=ALU.mult)
+        nc.vector.tensor_copy(out=ki[:], in_=un[:])
+        nc.vector.tensor_copy(out=kf[:], in_=ki[:])
+        nc.vector.tensor_tensor(out=un[:], in0=un[:], in1=kf[:], op=ALU.subtract)
+        nc.vector.scalar_tensor_tensor(out=un[:], in0=posf[:], scalar=fk[:, 1:2], in1=un[:], op0=ALU.mult, op1=ALU.add)
+        nc.vector.scalar_tensor_tensor(out=na[:], in0=un[:, 0:P + 2 * CH], scalar=0.5, in1=un[:, 0:P + 2 * CH],
+                                       op0=ALU.is_ge, op1=ALU.subtract)
+        nc.vector.scalar_tensor_tensor(out=nb1[:], in0=un[:, CC], scalar=0.0, in1=un[:, CC], op0=ALU.is_lt, op1=ALU.add)
+        nc.vector.scalar_tensor_tensor(out=nb[:], in0=nb1[:], scalar=1.0, in1=nb1[:], op0=ALU.is_ge, op1=ALU.subtract)
+
+        w32 = w_sb[:].bitcast(F32)
+        gw = consts.tile([P, WCOLS * 4], BF16, name="gw", align_bytes=64)
         wc = consts.tile([P, WCOLS], U32, name="wc", align_bytes=64)
         ws = consts.tile([P, WCOLS], U8, name="ws", align_bytes=64)
-        xc = consts.tile([P, NT * P], U32, name="xc", align_bytes=64)
-        xs = consts.tile([P, NT * P], U8, name="xs", align_bytes=64)
-        base = consts.tile([P, NT, 2 * NPAIR], F32, name="base")
-        qtab = consts.tile([P, NT, 2 * DH], F32, name="qtab")
+        gwf = gw[:].bitcast(F32).rearrange("p (c u) -> p c u", u=2)
+        gwb = gw[:].rearrange("p (i e u f) -> p e i u f", e=2, u=2, f=2)
 
-        x32 = {}
+        def w_transposes(dst, slot, r):
+            for u in range(2):
+                nc.tensor.transpose(dst[:, slot + u, :], w32[:, r, u:2 * P:2], ident[:])
+
+        def quant_w(lo, hi):
+            nc.vector.quantize_mx(out=wc[:, lo:hi].bitcast(FP8X4), scales=ws[:, lo:hi], in_=gw[:, 4 * lo:4 * hi])
+
+        pa = bank("q0", [P, 4, P])
+        w_transposes(pa, 0, 0)
+        w_transposes(pa, 2, 1)
+        pb = bank("q1", [P, 2, P])
+        w_transposes(pb, 0, 2)
+        nc.scalar.copy(out=gwf[:, 256:512, :].rearrange("p (r c) u -> p r c u", r=2),
+                       in_=pa[:].rearrange("p (r u) c -> p r c u", u=2))
+        nc.scalar.copy(out=gwf[:, 576:704, :], in_=pb[:].rearrange("p u c -> p c u"))
+
         grp = {}
-
-        def bank(n, shape):
-            return psum.tile(shape, F32, name="b%d" % n)
-
-        def ev_bank(e):
-            c, b = divmod(e, 4)
-            if b == 0:
-                grp[c] = grps.tile([P, 4096], BF16, name="grp", align_bytes=64)
-            xt = bank(e % 4, [P, 4, P])
-            for a in range(2):
-                for u in range(2):
-                    nc.tensor.transpose(xt[:, 2 * a + u, :], x32[c][:, 2 * b + a, u:2 * P:2], ident[:])
-            grf = grp[c][:].bitcast(F32).rearrange("p (b a r u) -> p b a r u", b=4, a=2, u=2)
-            nc.scalar.copy(out=grf[:, b], in_=xt[:].rearrange("p (a u) r -> p a r u", u=2))
-
-        def qx(c):
-            cols = slice(c * CH * P, (c + 1) * CH * P)
-            nc.vector.quantize_mx(out=xc[:, cols].bitcast(FP8X4), scales=xs[:, cols], in_=grp[c][:])
-
-        def qgh(h):
-            js = slice(GR * h, GR * h + GR)
-            nc.vector.tensor_tensor(
-                out=qtab[:, js, :].rearrange("p j (c i e) -> p (j c) i e", c=2, e=2),
-                in0=base[:, js, :].rearrange("p j (c i) -> p (j c) i", c=2).unsqueeze(3).to_broadcast(
-                    [P, 2 * GR, NPAIR, 2]),
-                in1=gq[:].rearrange("p (i e) -> p i e", e=2).unsqueeze(1).to_broadcast([P, 2 * GR, NPAIR, 2]),
-                op=ALU.mult)
-
-        with tc.tile_pool(name="pro", bufs=1) as pro, tc.tile_pool(name="tabs", bufs=4) as tabs:
-            w_sb = pro.tile([P, 3, D], BF16, name="w_sb")
-            nc.scalar.dma_start(out=w_sb[:, 0:2, :], in_=wq.rearrange("(r p) k -> p r k", p=P))
-            nc.scalar.dma_start(out=w_sb[:, 2, :], in_=wkv)
-            nc.scalar.dma_start(out=gq_bf[:], in_=q_norm_w.partition_broadcast(P))
-            nc.scalar.dma_start(out=gk_bf[:], in_=k_norm_w.partition_broadcast(P))
-            for c in range(NCH):
-                x_sb = xin.tile([P, CH, D], BF16, name="x_sb")
-                nc.sync.dma_start(out=x_sb[:], in_=xv[:, c * CH:(c + 1) * CH, :])
-                x32[c] = x_sb[:].bitcast(F32)
-
-            make_identity(nc, ident[:])
-            t1i = pro.tile([P, NCH], I32, name="t1i")
-            nc.gpsimd.iota(t1i[:], pattern=[[CH, NCH]], base=0, channel_multiplier=NT)
-            j0i = pro.tile([P, CH], I32, name="j0i")
-            nc.gpsimd.iota(j0i[:], pattern=[[1, CH]], base=0, channel_multiplier=0)
-            nc.vector.memset(ones[:], 1.0)
-            nc.vector.memset(eps_t[:], EPS)
-            his, los = turn_constants()
-            fhi = pro.tile([P, NPAIR], F32, name="fhi")
-            flo = pro.tile([P, NPAIR], F32, name="flo")
-            for i in range(NPAIR):
-                nc.vector.memset(fhi[:, i:i + 1], his[i])
-                nc.scalar.activation(out=flo[:, i:i + 1], in_=ones[:], func=ACT.Copy, scale=los[i])
-            idv = ident[:].rearrange("p (i e) -> p e i", e=2)
-            pmv = perm[:].rearrange("p (i e) -> p e i", e=2)
-            nc.vector.tensor_copy(out=pmv[:, 0], in_=idv[:, 1])
-            nc.vector.tensor_copy(out=pmv[:, 1], in_=idv[:, 0])
-            t1f = pro.tile([P, NCH], F32, name="t1f")
-            j0f = pro.tile([P, CH], F32, name="j0f")
-            nc.vector.tensor_copy(out=t1f[:], in_=t1i[:])
-            nc.vector.tensor_copy(out=j0f[:], in_=j0i[:])
-
-            w32 = w_sb[:].bitcast(F32)
-            gw = pro.tile([P, WCOLS * 4], BF16, name="gw", align_bytes=64)
-            gwf = gw[:].bitcast(F32).rearrange("p (c u) -> p c u", u=2)
-            gwb = gw[:].rearrange("p (i e u f) -> p e i u f", e=2, u=2, f=2)
-
-            def w_transposes(dst, slot, r, mat):
-                for u in range(2):
-                    nc.tensor.transpose(dst[:, slot + u, :], w32[:, r, u:2 * P:2], mat[:])
-
-            def plain_cols(src, slot, cb):
-                nc.scalar.copy(out=gwf[:, cb:cb + P, :], in_=src[:, slot:slot + 2, :].rearrange("p u c -> p c u"))
-
-            def swapped_cols(src, slot, cb, n):
-                sv = src[:, slot:slot + 2, 0:n].rearrange("p u (i e) -> p e i u", e=2)
-                dv = gwf[:, cb:cb + n, :].rearrange("p (i e) u -> p e i u", e=2)
-                nc.vector.tensor_copy(out=dv[:, 1], in_=sv[:, 1])
-                sb = src[:].bitcast(BF16)[:, slot:slot + 2, 0:2 * n].rearrange("p u (i e f) -> p e i u f", e=2, f=2)
-                nc.vector.tensor_scalar(out=gwb[:, 0, cb // 2:(cb + n) // 2], in0=sb[:, 0], scalar1=-1.0,
-                                        scalar2=None, op0=ALU.mult)
-
-            pa = bank(4, [P, 4, P])
-            w_transposes(pa, 0, 0, ident)
-            w_transposes(pa, 2, 1, ident)
-            pb = bank(5, [P, 4, P])
-            w_transposes(pb, 0, 2, ident)
-            w_transposes(pb, 2, 2, perm)
-            pc = bank(6, [P, 4, P])
-            w_transposes(pc, 0, 0, perm)
-            w_transposes(pc, 2, 1, perm)
-            plain_cols(pa, 0, 256)
-            plain_cols(pa, 2, 384)
-            plain_cols(pb, 0, 576)
-
-            def outer(dst, col, row):
-                nc.vector.tensor_tensor(out=dst[:], in0=col[:].unsqueeze(2).to_broadcast([P, 8, NPAIR]),
-                                        in1=row[:].unsqueeze(1).to_broadcast([P, 8, NPAIR]), op=ALU.mult)
-
-            def flat(t):
-                return t[:].rearrange("p a i -> p (a i)")
-
-            uh = pro.tile([P, 8, NPAIR], F32, name="uh")
-            ki = pro.tile([P, 8, NPAIR], I32, name="ki")
-            kf = pro.tile([P, 8, NPAIR], F32, name="kf")
-            ul = pro.tile([P, 8, NPAIR], F32, name="ul")
-            na = pro.tile([P, 8, NPAIR], F32, name="na")
-            bh = pro.tile([P, 8, NPAIR], F32, name="bh")
-            bl = pro.tile([P, 8, NPAIR], F32, name="bl")
-            bb = pro.tile([P, 8, 2, NPAIR], F32, name="bb")
-            nb = pro.tile([P, 16, NPAIR], F32, name="nb")
-            bbf = bb[:].rearrange("p a c i -> p (a c i)")
-            outer(uh, t1f, fhi)
-            outer(bh, j0f, fhi)
-            nc.vector.tensor_copy(out=ki[:], in_=uh[:])
-            outer(bl, j0f, flo)
-            nc.vector.tensor_copy(out=kf[:], in_=ki[:])
-            outer(ul, t1f, flo)
-            nc.vector.tensor_tensor(out=uh[:], in0=uh[:], in1=kf[:], op=ALU.subtract)
-            nc.vector.tensor_tensor(out=bb[:, :, 0, :], in0=bh[:], in1=bl[:], op=ALU.add)
-            nc.vector.tensor_tensor(out=uh[:], in0=uh[:], in1=ul[:], op=ALU.add)
-            nc.vector.tensor_scalar(out=bb[:, :, 1, :], in0=bb[:, :, 0, :], scalar1=0.25, scalar2=None, op0=ALU.add)
-            nc.vector.scalar_tensor_tensor(out=flat(na), in0=flat(uh), scalar=0.5, in1=flat(uh), op0=ALU.is_ge,
-                                           op1=ALU.subtract)
-            nc.vector.scalar_tensor_tensor(out=flat(nb), in0=bbf, scalar=1.0, in1=bbf, op0=ALU.is_ge,
-                                           op1=ALU.subtract)
-
-            swapped_cols(pb, 2, 512, DH)
-            swapped_cols(pc, 0, 0, P)
-            swapped_cols(pc, 2, 128, P)
-
-            for e in range(9):
-                ev_bank(e)
-
-            for c in range(NCH):
-                nv = tabs.tile([P, 16, NPAIR], F32, name="nv")
-                nc.gpsimd.tensor_tensor(out=nv[:], in0=nb[:],
-                                        in1=na[:, c, :].unsqueeze(1).to_broadcast([P, 16, NPAIR]), op=ALU.add)
-                if c >= 2:
-                    qgh(c - 2)
-                nc.vector.scalar_tensor_tensor(out=flat(nv), in0=flat(nv), scalar=-0.5, in1=flat(nv), op0=ALU.is_lt,
-                                               op1=ALU.add)
-                if c == 0:
-                    nc.vector.quantize_mx(out=wc[:, 0:512].bitcast(FP8X4), scales=ws[:, 0:512], in_=gw[:, 0:2048])
-                    nc.vector.quantize_mx(out=wc[:, 512:640].bitcast(FP8X4), scales=ws[:, 512:640],
-                                          in_=gw[:, 2048:2560])
-                    nc.vector.quantize_mx(out=wc[:, 640:704].bitcast(FP8X4), scales=ws[:, 640:704],
-                                          in_=gw[:, 2560:2816])
-                    nc.vector.tensor_copy(out=gq[:], in_=gq_bf[:])
-                    nc.vector.tensor_copy(out=gk[:], in_=gk_bf[:])
-                nc.scalar.activation(out=base[:, c * CH:(c + 1) * CH, :].rearrange("p j m -> p (j m)"), in_=flat(nv),
-                                     func=ACT.Sin, scale=-TWO_PI)
-                ev_bank(9 + c)
-
-        for e in range(17, 32):
-            ev_bank(e)
-        for c in range(NCH):
-            qx(c)
-
-        work = ctx.enter_context(tc.tile_pool(name="work", bufs=2))
-        outs = ctx.enter_context(tc.tile_pool(name="outs", bufs=2))
-
+        xc_t = {}
+        xs_t = {}
+        base_t = {}
+        tab_t = {}
+        qtab_t = {}
         ps_t = {}
         ss_t = {}
         rs_t = {}
@@ -250,12 +190,75 @@ def tile_attention_pa_t_kernel(tc, x, wq, wkv, q_norm_w, k_norm_w, out_0, out_1,
         tk_t = {}
         pq_t = {}
         pk_t = {}
+        xt_t = {}
+        ring = [0]
+
+        def xbank(shape):
+            t = bank("x%d" % (ring[0] % 2), shape)
+            ring[0] += 1
+            return t
+
+        def transposes(g):
+            for b in range(2):
+                xt = xbank([P, 4, P])
+                xt_t[2 * g + b] = xt
+                for a in range(2):
+                    for u in range(2):
+                        nc.tensor.transpose(xt[:, 2 * a + u, :], x32[g][:, 2 * b + a, u:2 * P:2], ident[:])
+
+        def evac(g, b, on_vector=False):
+            if b == 0:
+                grp[g] = grps.tile([P, GR * D], BF16, name="grp", align_bytes=64)
+            grf = grp[g][:].bitcast(F32).rearrange("p (b a r u) -> p b a r u", b=2, a=2, u=2)
+            src = xt_t[2 * g + b][:].rearrange("p (a u) r -> p a r u", u=2)
+            if on_vector:
+                nc.vector.tensor_copy(out=grf[:, b], in_=src)
+            else:
+                nc.scalar.copy(out=grf[:, b], in_=src)
+
+        def quant(g):
+            xc_t[g] = codes.tile([P, GR * P], U32, name="xc", align_bytes=64)
+            xs_t[g] = codes.tile([P, GR * P], U8, name="xs", align_bytes=64)
+            nc.vector.quantize_mx(out=xc_t[g][:].bitcast(FP8X4), scales=xs_t[g][:], in_=grp[g][:])
+
+        nv = consts.tile([P, CH, P], F32, name="nv")
+        nv2 = consts.tile([P, CH, P], F32, name="nv2")
+        ac = consts.tile([P, CH, P], F32, name="ac")
+
+        def flat(t, lo, hi):
+            return t[:, lo:hi, :].rearrange("p c n -> p (c n)")
+
+        def angles(lo, hi):
+            for c in range(lo, hi):
+                nc.vector.tensor_scalar(out=nv[:, c, :], in0=na[:, 0:P], scalar1=nb[:, c:c + 1], scalar2=None,
+                                        op0=ALU.add)
+            nc.vector.scalar_tensor_tensor(out=flat(nv2, lo, hi), in0=flat(nv, lo, hi), scalar=-0.5,
+                                           in1=flat(nv, lo, hi), op0=ALU.is_lt, op1=ALU.add)
+            nc.scalar.activation(out=flat(ac, lo, hi), in_=flat(nv2, lo, hi), func=ACT.Sin, scale=-TWO_PI)
+
+        def table(c):
+            tb = xbank([P, CH, 2 * NPAIR])
+            tab_t[c] = tb
+            nc.tensor.matmul(out=tb[:].rearrange("p j m -> p (j m)"), lhsT=ac[:, c, :], rhs=brow[:], start=True, stop=True)
+            base_t[c] = tabs.tile([P, CH, 2 * NPAIR], F32, name="base")
+            nc.scalar.copy(out=base_t[c][:], in_=tb[:])
+
+        def qgain(g, src):
+            half = slice(GR * (g % 2), GR * (g % 2) + GR)
+            qtab_t[g] = tabs.tile([P, GR, 2 * DH], F32, name="qtab")
+            nc.vector.tensor_tensor(
+                out=qtab_t[g][:].rearrange("p j (m e) -> p j m e", e=2),
+                in0=src[:, half, :].unsqueeze(3).to_broadcast([P, GR, 2 * NPAIR, 2]),
+                in1=gg[:].rearrange("p (m e) -> p m e", e=2).unsqueeze(1).to_broadcast([P, GR, 2 * NPAIR, 2]),
+                op=ALU.mult)
 
         def lhs_of(j):
-            return xc[:, j * P:(j + 1) * P].bitcast(FP8X4), xs[:, j * P:(j + 1) * P]
+            g, i = divmod(j, GR)
+            cols = slice(i * P, (i + 1) * P)
+            return xc_t[g][:, cols].bitcast(FP8X4), xs_t[g][:, cols]
 
         def m1(j):
-            ps = bank(4 + j % 3, [P, 384])
+            ps = bank("a%d" % (j % 2), [P, 384])
             ps_t[j] = ps
             lhs, lsc = lhs_of(j)
             nc.tensor.matmul_mx(out=ps[:, 0:256], lhsT=lhs, lhsT_scale=lsc, rhs=wc[:, 256:512].bitcast(FP8X4),
@@ -264,116 +267,183 @@ def tile_attention_pa_t_kernel(tc, x, wq, wkv, q_norm_w, k_norm_w, out_0, out_1,
                                 rhs_scale=ws[:, 576:704], start=True, stop=True)
 
         def squares(j):
-            q, i = divmod(j, GR)
+            g, i = divmod(j, GR)
             c, jj = divmod(j, CH)
             if i == 0:
-                ss_t[q] = small.tile([P, 5 * GR], F32, name="ss")
+                ss_t[g] = small.tile([P, 5 * GR], F32, name="ss")
             if jj == 0:
-                ov_t[c] = outs.tile([P, CH, DH], F32, name="ov", bufs=3)
+                ov_t[c] = outs.tile([P, CH, DH], F32, name="ov")
             ps = ps_t[j]
             junk = junks.tile([P, 5, DH], BF16, name="junk")
             for h in range(5):
                 nc.scalar.activation(out=junk[:, h, :], in_=ps[:, h * DH:(h + 1) * DH], func=ACT.Square,
-                                     accum_out=ss_t[q][:, i * 5 + h:i * 5 + h + 1])
+                                     accum_out=ss_t[g][:, i * 5 + h:i * 5 + h + 1])
             nc.scalar.copy(out=ov_t[c][:, jj, :], in_=ps[:, 320:384])
             if i == GR - 1:
-                rs_t[q] = small.tile([P, 5 * GR], F32, name="rs")
-                nc.scalar.activation(out=rs_t[q][:], in_=ss_t[q][:], func=ACT.Abs_reciprocal_sqrt, scale=1.0 / DH,
+                rs_t[g] = small.tile([P, 5 * GR], F32, name="rs")
+                nc.scalar.activation(out=rs_t[g][:], in_=ss_t[g][:], func=ACT.Abs_reciprocal_sqrt, scale=1.0 / DH,
                                      bias=eps_t[:])
+            if jj == CH - 1:
+                nc.sync.dma_start(out=ovv[:, c * CH:(c + 1) * CH, :], in_=ov_t[c][:])
 
         def m2q(j):
-            pq = bank(j % 4, [P, 512])
+            pq = bank("q%d" % (j % 3), [P, 512])
             pq_t[j] = pq
             lhs, lsc = lhs_of(j)
             nc.tensor.matmul_mx(out=pq[:], lhsT=lhs, lhsT_scale=lsc, rhs=wc[:, 0:512].bitcast(FP8X4),
                                 rhs_scale=ws[:, 0:512], start=True, stop=True)
 
-        def m2k(q):
-            pk = bank(7, [P, GR, 2 * DH])
-            pk_t[q] = pk
+        def m2k(g):
+            pk = bank("k0", [P, GR, 2 * DH])
+            pk_t[g] = pk
             for i in range(GR):
-                lhs, lsc = lhs_of(q * GR + i)
+                lhs, lsc = lhs_of(g * GR + i)
                 nc.tensor.matmul_mx(out=pk[:, i, :], lhsT=lhs, lhsT_scale=lsc, rhs=wc[:, 512:640].bitcast(FP8X4),
                                     rhs_scale=ws[:, 512:640], start=True, stop=True)
 
-        def rope(j):
-            q, i = divmod(j, GR)
-            c, jj = divmod(j, CH)
-            if i == 0:
-                tq_t[q] = work.tile([P, GR, 512], F32, name="tq", bufs=3)
-            if jj == 0:
-                tk_t[c] = work.tile([P, CH, 2 * DH], F32, name="tk")
-            rs = rs_t[q]
-            pv = pq_t[j][:].rearrange("p (c h d) -> p h c d", c=2, h=4)
-            tv = tq_t[q][:, i, :].rearrange("p (c h d) -> p h c d", c=2, h=4)
-            for h in range(4):
-                nc.vector.scalar_tensor_tensor(out=tv[:, h], in0=pv[:, h], scalar=rs[:, i * 5 + h:i * 5 + h + 1],
-                                               in1=qtab[:, j, :].rearrange("p (c d) -> p c d", c=2), op0=ALU.mult,
-                                               op1=ALU.mult)
-            nc.vector.scalar_tensor_tensor(
-                out=tk_t[c][:, jj, :].rearrange("p (m e) -> p m e", e=2),
-                in0=pk_t[q][:, i, :].rearrange("p (m e) -> p m e", e=2), scalar=rs[:, i * 5 + 4:i * 5 + 5],
-                in1=base[:, j, :].unsqueeze(2).to_broadcast([P, 2 * NPAIR, 2]), op0=ALU.mult, op1=ALU.mult)
+        def rope_k(g):
+            c, half = divmod(g, 2)
+            tk_t[g] = work.tile([P, GR, 2 * DH], F32, name="tk")
+            for i in range(GR):
+                nc.vector.scalar_tensor_tensor(
+                    out=tk_t[g][:, i, :].rearrange("p (m e) -> p m e", e=2),
+                    in0=pk_t[g][:, i, :].rearrange("p (m e) -> p m e", e=2), scalar=rs_t[g][:, i * 5 + 4:i * 5 + 5],
+                    in1=base_t[c][:, half * GR + i, :].unsqueeze(2).to_broadcast([P, 2 * NPAIR, 2]), op0=ALU.mult,
+                    op1=ALU.mult)
 
-        def add_q(eng, q, lo, hi):
-            c, half = divmod(q, 2)
+        def rope_q(j):
+            g, i = divmod(j, GR)
+            if i == 0:
+                tq_t[g] = work.tile([P, GR, 512], F32, name="tq")
+            pv = pq_t[j][:].rearrange("p (c h d) -> p h c d", c=2, h=4)
+            tv = tq_t[g][:, i, :].rearrange("p (c h d) -> p h c d", c=2, h=4)
+            for h in range(4):
+                nc.vector.scalar_tensor_tensor(out=tv[:, h], in0=pv[:, h], scalar=rs_t[g][:, i * 5 + h:i * 5 + h + 1],
+                                               in1=qtab_t[g][:, i, :].rearrange("p (c d) -> p c d", c=2), op0=ALU.mult,
+                                               op1=ALU.mult)
+
+        def add_q(eng, g, lo, hi):
+            c, half = divmod(g, 2)
             if half == 0 and lo == 0:
                 oq_t[c] = outs.tile([P, 4, CH, DH], F32, name="oq")
-            tq = tq_t[q]
+            tq = tq_t[g]
             eng.tensor_tensor(
                 out=oq_t[c][:, :, half * GR + lo:half * GR + hi, :].rearrange("p h j d -> p j h d"),
                 in0=tq[:, lo:hi, 0:256].rearrange("p j (h d) -> p j h d", h=4),
                 in1=tq[:, lo:hi, 256:512].rearrange("p j (h d) -> p j h d", h=4), op=ALU.add)
 
-        def add_k(c, lo, hi):
-            if lo == 0:
+        def add_k(g):
+            c, half = divmod(g, 2)
+            if half == 0:
                 ok_t[c] = outs.tile([P, CH, DH], F32, name="ok")
-            uk = work.tile([P, CH, DH], F32, name="uk")
-            nc.gpsimd.tensor_tensor(out=uk[:, lo:hi, :], in0=tk_t[c][:, lo:hi, 0:DH], in1=tk_t[c][:, lo:hi, DH:2 * DH],
-                                    op=ALU.add)
-            nc.gpsimd.tensor_tensor(out=ok_t[c][:, lo:hi, :], in0=uk[:, lo:hi, :],
-                                    in1=gk[:].unsqueeze(1).to_broadcast([P, hi - lo, DH]), op=ALU.mult)
+            uk = work.tile([P, GR, DH], F32, name="uk")
+            nc.gpsimd.tensor_tensor(out=uk[:], in0=tk_t[g][:, :, 0:DH], in1=tk_t[g][:, :, DH:2 * DH], op=ALU.add)
+            nc.gpsimd.tensor_tensor(out=ok_t[c][:, half * GR:half * GR + GR, :], in0=uk[:],
+                                    in1=gk[:].unsqueeze(1).to_broadcast([P, GR, DH]), op=ALU.mult)
 
-        def store(c, lo, hi):
+        def store_q(c, lo, hi):
             js = slice(c * CH + lo, c * CH + hi)
             nc.sync.dma_start(out=oqv[:, :, js, :], in_=oq_t[c][:, :, lo:hi, :])
-            nc.sync.dma_start(out=okv[:, js, :], in_=ok_t[c][:, lo:hi, :])
 
-        for a in range(D1):
-            m1(a)
-        for a in range(SL):
-            m1(a + D1)
-            squares(a)
+        def store_k(c):
+            nc.sync.dma_start(out=okv[:, c * CH:(c + 1) * CH, :], in_=ok_t[c][:])
+
+        transposes(0)
+        evac(0, 0)
+        evac(0, 1)
+        nc.scalar.activation(out=vr[:], in_=na[:, P:P + 2 * CH], func=ACT.Sin, scale=-TWO_PI)
+        nc.gpsimd.tensor_tensor(out=brow[:].rearrange("p (m i) -> p m i", i=NPAIR),
+                                in0=vr[:].unsqueeze(2).to_broadcast([P, 2 * CH, NPAIR]),
+                                in1=mask[:].unsqueeze(1).to_broadcast([P, 2 * CH, NPAIR]), op=ALU.mult)
+        quant_w(256, 512)
+        quant_w(576, 704)
+        angles(0, 1)
+        quant(0)
+        m1(0)
+        m1(1)
+        angles(1, NCH)
+        nc.scalar.activation(out=warm[:, 1:2], in_=ones[:], func=ACT.Abs_reciprocal_sqrt)
+
+        pav = pa[:].rearrange("p (r u) (i e) -> p e r i u", u=2, e=2)
+        gqv = gwf[:, 0:256, :].rearrange("p (r i e) u -> p e r i u", r=2, e=2)
+        nc.vector.tensor_copy(out=gqv[:, 0], in_=pav[:, 1])
+        nc.vector.tensor_copy(out=gqv[:, 1], in_=pav[:, 0])
+        pbv = pb[:, :, 0:DH].rearrange("p u (i e) -> p e i u", e=2)
+        gkv = gwf[:, 512:576, :].rearrange("p (i e) u -> p e i u", e=2)
+        nc.vector.tensor_copy(out=gkv[:, 1], in_=pbv[:, 0])
+        pbb = pb[:].bitcast(BF16)[:, :, 0:2 * DH].rearrange("p u (i e f) -> p e i u f", e=2, f=2)
+        nc.vector.tensor_scalar(out=gwb[:, 0, 256:288], in0=pbb[:, 1], scalar1=-1.0, scalar2=None, op0=ALU.mult)
+        quant_w(0, 256)
+        quant_w(512, 576)
+
+        pg = bank("q2", [P, 2 * DH])
+        nc.tensor.matmul(out=pg[:], lhsT=ones_bf[:], rhs=gains[:], start=True, stop=True)
+        gg = consts.tile([P, 2 * DH], F32, name="gg")
+        gk = consts.tile([P, DH], F32, name="gk")
+        nc.vector.tensor_copy(out=gg[:, DH:2 * DH], in_=pg[:, 0:DH])
+        ggs = gg[:, 0:DH].rearrange("p (i e) -> p e i", e=2)
+        pgs = pg[:, 0:DH].rearrange("p (i e) -> p e i", e=2)
+        nc.vector.tensor_scalar(out=ggs[:, 0], in0=pgs[:, 0], scalar1=-1.0, scalar2=None, op0=ALU.mult)
+        nc.vector.tensor_copy(out=ggs[:, 1], in_=pgs[:, 1])
+        nc.vector.tensor_copy(out=gk[:], in_=pg[:, DH:2 * DH])
+
+        transposes(1)
+        evac(1, 0)
+        evac(1, 1)
+        table(0)
+        quant(1)
+        transposes(2)
+        for i in range(GR):
+            m1(i + D1)
+            squares(i)
+            if i < 2:
+                evac(2, i)
+            if i == 1:
+                qgain(0, tab_t[0])
+                qgain(1, base_t[0])
         for j in range(D2):
             m2q(j)
         m2k(0)
 
-        for q in range(NGR):
-            if 6 + q < NGR:
-                qgh(6 + q)
+        for g in range(NG):
+            c, half = divmod(g, 2)
+            if g + 3 < NG:
+                transposes(g + 3)
+            rope_k(g)
             for i in range(GR):
-                j = q * GR + i
-                a = j + SL
-                if a + D1 < NT:
-                    m1(a + D1)
-                if i == 0 and q > 0:
-                    m2k(q)
+                j = GR * g + i
+                s = j + GR
+                if i == 1 and g + 2 < NG:
+                    quant(g + 2)
+                if s + D1 < NT:
+                    m1(s + D1)
+                if i == 1 and g + 1 < NG:
+                    m2k(g + 1)
                 if j + D2 < NT:
                     m2q(j + D2)
-                if a < NT:
-                    squares(a)
-                    if a % CH == CH - 1:
-                        nc.sync.dma_start(out=ovv[:, a - CH + 1:a + 1, :], in_=ov_t[a // CH][:])
-                rope(j)
-            c = q // 2
-            add_q(nc.vector if (q % 4 == 3 or q >= NGR - 2) else nc.gpsimd, q, 0, GR)
-            if q < NGR - 2:
-                if q % 2 == 1:
-                    add_k(c, 0, CH)
-                    store(c, 0, CH)
-            elif q == NGR - 2:
-                add_k(c, 0, GR)
-                store(c, 0, GR)
+                if s < NT:
+                    squares(s)
+                if g + 3 < NG and i < 2:
+                    evac(g + 3, i)
+                rope_q(j)
+                if i == 1 and half == 0 and c + 1 < NCH:
+                    table(c + 1)
+                if i == 3 and c + 1 < NCH:
+                    if half == 0:
+                        qgain(g + 2, tab_t[c + 1])
+                    else:
+                        qgain(g + 2, base_t[c + 1])
+                if g == NG - 1 and i == 1:
+                    add_q(nc.gpsimd, g, 0, 2)
+                    add_k(g)
+                    store_q(c, 0, GR + 2)
+                    store_k(c)
+            if g == NG - 1:
+                add_q(nc.vector, g, 2, GR)
+                store_q(c, GR + 2, CH)
             else:
-                add_k(c, GR, CH)
-                store(c, GR, CH)
+                add_q(nc.vector if g in VECTOR_ADDS else nc.gpsimd, g, 0, GR)
+                add_k(g)
+                if half == 1:
+                    store_q(c, 0, CH)
+                    store_k(c)

@@ -24,8 +24,12 @@ CH = 8
 NCH = 8
 GR = 4
 NG = 16
-D1 = 2
-D2 = 3
+LS = 6
+NA = 3
+ND = 5
+PA = 3
+PD = 5
+TABV = 2
 EPS = 1.1920929e-07
 TWO_PI = 6.283185307179586
 WCOLS = 704
@@ -87,11 +91,10 @@ def tile_attention_pa_t_kernel(tc, x, wq, wkv, q_norm_w, k_norm_w, out_0, out_1,
         make_identity(nc, ident[:])
         kpi = consts.tile([P, 1], I32, name="kpi")
         nc.gpsimd.iota(kpi[:], pattern=[[0, 1]], base=0, channel_multiplier=1)
-        NPOS = P + 3 * CH
+        NPOS = P + 2 * NT
         posi = consts.tile([P, NPOS], I32, name="posi")
         nc.gpsimd.iota(posi[:, 0:P], pattern=[[NT, P]], base=0, channel_multiplier=0)
-        nc.gpsimd.iota(posi[:, P:P + 2 * CH], pattern=[[1, CH], [0, 2]], base=0, channel_multiplier=0)
-        nc.gpsimd.iota(posi[:, P + 2 * CH:NPOS], pattern=[[CH, CH]], base=0, channel_multiplier=0)
+        nc.gpsimd.iota(posi[:, P:NPOS], pattern=[[1, NT], [0, 2]], base=0, channel_multiplier=0)
         ones = consts.tile([P, 1], F32, name="ones")
         eps_t = consts.tile([P, 1], F32, name="eps_t")
         ones_bf = consts.tile([P, P], BF16, name="ones_bf")
@@ -116,14 +119,8 @@ def tile_attention_pa_t_kernel(tc, x, wq, wkv, q_norm_w, k_norm_w, out_0, out_1,
         fk = consts.tile([P, 2], F32, name="fk")
         un = consts.tile([P, NPOS], F32, name="un")
         ki = consts.tile([P, NPOS], I32, name="ki")
-        kf = consts.tile([P, NPOS], F32, name="kf")
-        na = consts.tile([P, P + 2 * CH], F32, name="na")
-        nb = consts.tile([P, CH], F32, name="nb")
-        nb1 = consts.tile([P, CH], F32, name="nb1")
-        vr = consts.tile([P, 2 * CH], F32, name="vr")
-        brow = consts.tile([P, CH * 2 * NPAIR], F32, name="brow")
-        RC = slice(P, P + 2 * CH)
-        CC = slice(P + 2 * CH, NPOS)
+        na = consts.tile([P, NPOS], F32, name="na")
+        trig = consts.tile([P, NPOS], F32, name="trig")
         nc.vector.tensor_copy(out=kpf[:], in_=kpi[:])
         nc.vector.tensor_copy(out=posf[:], in_=posi[:])
         nc.vector.tensor_scalar(out=s4[:], in0=kpf[:], scalar1=float(NPAIR), scalar2=0.25, op0=ALU.is_ge, op1=ALU.mult)
@@ -133,23 +130,14 @@ def tile_attention_pa_t_kernel(tc, x, wq, wkv, q_norm_w, k_norm_w, out_0, out_1,
         nc.vector.tensor_tensor(out=fsel[:], in0=frow[:], in1=mask[:].unsqueeze(1).to_broadcast([P, 2, NPAIR]),
                                 op=ALU.mult)
         nc.vector.tensor_reduce(out=fk[:], in_=fsel[:], op=ALU.add, axis=AX.X)
-        nc.vector.tensor_scalar(out=un[:, 0:P], in0=posf[:, 0:P], scalar1=fk[:, 0:1], scalar2=php[:], op0=ALU.mult,
-                                op1=ALU.add)
-        unr = un[:, RC].rearrange("p (r c) -> p c r", c=2)
-        por = posf[:, RC].rearrange("p (r c) -> p c r", c=2)
-        nc.vector.tensor_scalar(out=unr[:, 0], in0=por[:, 0], scalar1=fk[:, 0:1], scalar2=s4[:], op0=ALU.mult,
-                                op1=ALU.add)
-        nc.vector.tensor_scalar(out=unr[:, 1], in0=por[:, 1], scalar1=fk[:, 0:1], scalar2=phr[:], op0=ALU.mult,
-                                op1=ALU.add)
-        nc.vector.tensor_scalar(out=un[:, CC], in0=posf[:, CC], scalar1=fk[:, 0:1], scalar2=None, op0=ALU.mult)
-        nc.vector.tensor_copy(out=ki[:], in_=un[:])
-        nc.vector.tensor_copy(out=kf[:], in_=ki[:])
-        nc.vector.tensor_tensor(out=un[:], in0=un[:], in1=kf[:], op=ALU.subtract)
+        por = posf[:, P:NPOS].rearrange("p (r c) -> p c r", c=2)
+        for dst in (ki, un):
+            dsr = dst[:, P:NPOS].rearrange("p (r c) -> p c r", c=2)
+            for o, src, phase in ((dst[:, 0:P], posf[:, 0:P], php), (dsr[:, 0], por[:, 0], s4), (dsr[:, 1], por[:, 1], phr)):
+                nc.vector.tensor_scalar(out=o, in0=src, scalar1=fk[:, 0:1], scalar2=phase[:], op0=ALU.mult, op1=ALU.add)
+        nc.vector.tensor_tensor(out=un[:], in0=un[:], in1=ki[:], op=ALU.subtract)
         nc.vector.scalar_tensor_tensor(out=un[:], in0=posf[:], scalar=fk[:, 1:2], in1=un[:], op0=ALU.mult, op1=ALU.add)
-        nc.vector.scalar_tensor_tensor(out=na[:], in0=un[:, 0:P + 2 * CH], scalar=0.5, in1=un[:, 0:P + 2 * CH],
-                                       op0=ALU.is_ge, op1=ALU.subtract)
-        nc.vector.scalar_tensor_tensor(out=nb1[:], in0=un[:, CC], scalar=0.0, in1=un[:, CC], op0=ALU.is_lt, op1=ALU.add)
-        nc.vector.scalar_tensor_tensor(out=nb[:], in0=nb1[:], scalar=1.0, in1=nb1[:], op0=ALU.is_ge, op1=ALU.subtract)
+        nc.vector.scalar_tensor_tensor(out=na[:], in0=un[:], scalar=0.5, in1=un[:], op0=ALU.is_ge, op1=ALU.subtract)
 
         w32 = w_sb[:].bitcast(F32)
         gw = consts.tile([P, WCOLS * 4], BF16, name="gw", align_bytes=64)
@@ -165,10 +153,10 @@ def tile_attention_pa_t_kernel(tc, x, wq, wkv, q_norm_w, k_norm_w, out_0, out_1,
         def quant_w(lo, hi):
             nc.vector.quantize_mx(out=wc[:, lo:hi].bitcast(FP8X4), scales=ws[:, lo:hi], in_=gw[:, 4 * lo:4 * hi])
 
-        pa = bank("q0", [P, 4, P])
+        pa = bank("d4", [P, 4, P])
         w_transposes(pa, 0, 0)
         w_transposes(pa, 2, 1)
-        pb = bank("q1", [P, 2, P])
+        pb = bank("d3", [P, 2, P])
         w_transposes(pb, 0, 2)
         nc.scalar.copy(out=gwf[:, 256:512, :].rearrange("p (r c) u -> p r c u", r=2),
                        in_=pa[:].rearrange("p (r u) c -> p r c u", u=2))
@@ -191,20 +179,19 @@ def tile_attention_pa_t_kernel(tc, x, wq, wkv, q_norm_w, k_norm_w, out_0, out_1,
         pq_t = {}
         pk_t = {}
         xt_t = {}
-        ring = [0]
+        turn = {"a": 0, "d": 0}
 
-        def xbank(shape):
-            t = bank("x%d" % (ring[0] % 2), shape)
-            ring[0] += 1
+        def next_bank(ring, shape):
+            t = bank("%s%d" % (ring, turn[ring] % (NA if ring == "a" else ND)), shape)
+            turn[ring] += 1
             return t
 
-        def transposes(g):
-            for b in range(2):
-                xt = xbank([P, 4, P])
-                xt_t[2 * g + b] = xt
-                for a in range(2):
-                    for u in range(2):
-                        nc.tensor.transpose(xt[:, 2 * a + u, :], x32[g][:, 2 * b + a, u:2 * P:2], ident[:])
+        def transposes(g, b):
+            xt = next_bank("a", [P, 4, P])
+            xt_t[2 * g + b] = xt
+            for a in range(2):
+                for u in range(2):
+                    nc.tensor.transpose(xt[:, 2 * a + u, :], x32[g][:, 2 * b + a, u:2 * P:2], ident[:])
 
         def evac(g, b, on_vector=False):
             if b == 0:
@@ -221,32 +208,24 @@ def tile_attention_pa_t_kernel(tc, x, wq, wkv, q_norm_w, k_norm_w, out_0, out_1,
             xs_t[g] = codes.tile([P, GR * P], U8, name="xs", align_bytes=64)
             nc.vector.quantize_mx(out=xc_t[g][:].bitcast(FP8X4), scales=xs_t[g][:], in_=grp[g][:])
 
-        nv = consts.tile([P, CH, P], F32, name="nv")
-        nv2 = consts.tile([P, CH, P], F32, name="nv2")
-        ac = consts.tile([P, CH, P], F32, name="ac")
+        brow_t = {}
 
-        def flat(t, lo, hi):
-            return t[:, lo:hi, :].rearrange("p c n -> p (c n)")
-
-        def angles(lo, hi):
-            for c in range(lo, hi):
-                nc.vector.tensor_scalar(out=nv[:, c, :], in0=na[:, 0:P], scalar1=nb[:, c:c + 1], scalar2=None,
-                                        op0=ALU.add)
-            nc.vector.scalar_tensor_tensor(out=flat(nv2, lo, hi), in0=flat(nv, lo, hi), scalar=-0.5,
-                                           in1=flat(nv, lo, hi), op0=ALU.is_lt, op1=ALU.add)
-            nc.scalar.activation(out=flat(ac, lo, hi), in_=flat(nv2, lo, hi), func=ACT.Sin, scale=-TWO_PI)
+        def table_rows(c):
+            brow_t[c] = tabs.tile([P, CH * 2 * NPAIR], F32, name="brow", bufs=NCH)
+            cols = slice(P + 2 * CH * c, P + 2 * CH * c + 2 * CH)
+            nc.gpsimd.tensor_tensor(out=brow_t[c][:].rearrange("p (m i) -> p m i", i=NPAIR),
+                                    in0=trig[:, cols].unsqueeze(2).to_broadcast([P, 2 * CH, NPAIR]),
+                                    in1=mask[:].unsqueeze(1).to_broadcast([P, 2 * CH, NPAIR]), op=ALU.mult)
 
         def table(c):
-            tb = xbank([P, CH, 2 * NPAIR])
+            tb = next_bank("d", [P, CH, 2 * NPAIR])
             tab_t[c] = tb
-            nc.tensor.matmul(out=tb[:].rearrange("p j m -> p (j m)"), lhsT=ac[:, c, :], rhs=brow[:], start=True, stop=True)
-            base_t[c] = tabs.tile([P, CH, 2 * NPAIR], F32, name="base")
-            nc.scalar.copy(out=base_t[c][:], in_=tb[:])
+            nc.tensor.matmul(out=tb[:].rearrange("p j m -> p (j m)"), lhsT=trig[:, 0:P], rhs=brow_t[c][:], start=True, stop=True)
 
-        def qgain(g, src):
+        def qgain(g, src, eng):
             half = slice(GR * (g % 2), GR * (g % 2) + GR)
             qtab_t[g] = tabs.tile([P, GR, 2 * DH], F32, name="qtab")
-            nc.vector.tensor_tensor(
+            eng.tensor_tensor(
                 out=qtab_t[g][:].rearrange("p j (m e) -> p j m e", e=2),
                 in0=src[:, half, :].unsqueeze(3).to_broadcast([P, GR, 2 * NPAIR, 2]),
                 in1=gg[:].rearrange("p (m e) -> p m e", e=2).unsqueeze(1).to_broadcast([P, GR, 2 * NPAIR, 2]),
@@ -258,7 +237,7 @@ def tile_attention_pa_t_kernel(tc, x, wq, wkv, q_norm_w, k_norm_w, out_0, out_1,
             return xc_t[g][:, cols].bitcast(FP8X4), xs_t[g][:, cols]
 
         def m1(j):
-            ps = bank("a%d" % (j % 2), [P, 384])
+            ps = next_bank("a", [P, 384])
             ps_t[j] = ps
             lhs, lsc = lhs_of(j)
             nc.tensor.matmul_mx(out=ps[:, 0:256], lhsT=lhs, lhsT_scale=lsc, rhs=wc[:, 256:512].bitcast(FP8X4),
@@ -287,14 +266,14 @@ def tile_attention_pa_t_kernel(tc, x, wq, wkv, q_norm_w, k_norm_w, out_0, out_1,
                 nc.sync.dma_start(out=ovv[:, c * CH:(c + 1) * CH, :], in_=ov_t[c][:])
 
         def m2q(j):
-            pq = bank("q%d" % (j % 3), [P, 512])
+            pq = next_bank("d", [P, 512])
             pq_t[j] = pq
             lhs, lsc = lhs_of(j)
             nc.tensor.matmul_mx(out=pq[:], lhsT=lhs, lhsT_scale=lsc, rhs=wc[:, 0:512].bitcast(FP8X4),
                                 rhs_scale=ws[:, 0:512], start=True, stop=True)
 
         def m2k(g):
-            pk = bank("k0", [P, GR, 2 * DH])
+            pk = next_bank("d", [P, GR, 2 * DH])
             pk_t[g] = pk
             for i in range(GR):
                 lhs, lsc = lhs_of(g * GR + i)
@@ -348,36 +327,88 @@ def tile_attention_pa_t_kernel(tc, x, wq, wkv, q_norm_w, k_norm_w, out_0, out_1,
         def store_k(c):
             nc.sync.dma_start(out=okv[:, c * CH:(c + 1) * CH, :], in_=ok_t[c][:])
 
-        transposes(0)
-        evac(0, 0)
-        evac(0, 1)
-        nc.scalar.activation(out=vr[:], in_=na[:, P:P + 2 * CH], func=ACT.Sin, scale=-TWO_PI)
-        nc.gpsimd.tensor_tensor(out=brow[:].rearrange("p (m i) -> p m i", i=NPAIR),
-                                in0=vr[:].unsqueeze(2).to_broadcast([P, 2 * CH, NPAIR]),
-                                in1=mask[:].unsqueeze(1).to_broadcast([P, 2 * CH, NPAIR]), op=ALU.mult)
+        d_items = [("t", 0)]
+        a_items = [("x", 0), ("x", 1), ("a", 0), ("a", 1), ("x", 2), ("x", 3), ("a", 2), ("a", 3), ("x", 4), ("a", 4),
+                   ("x", 5), ("a", 5), ("x", 6), ("x", 7)]
+        a_head = len(a_items)
+        a_at = {}
+        d_at = {}
+        for v in range(NT):
+            n0, m0 = len(a_items), len(d_items)
+            if v + LS < NT:
+                a_items.append(("a", v + LS))
+            xg, xr = divmod(v + 15, GR)
+            if xr % 2 == 0 and xg < NG:
+                a_items.append(("x", 2 * xg + xr // 2))
+            if v % GR == 0:
+                d_items.append(("k", v // GR))
+            d_items.append(("q", v))
+            if v % CH == TABV and v // CH + 1 < NCH:
+                d_items.append(("t", v // CH + 1))
+            a_at[v] = (n0, len(a_items))
+            d_at[v] = (m0, len(d_items))
+        made = {"a": 0, "d": 0}
+
+        def make(ring, upto):
+            items = a_items if ring == "a" else d_items
+            while made[ring] < min(upto, len(items)):
+                kind, n = items[made[ring]]
+                made[ring] += 1
+                if kind == "a":
+                    m1(n)
+                elif kind == "x":
+                    transposes(n // 2, n % 2)
+                elif kind == "k":
+                    m2k(n)
+                elif kind == "q":
+                    m2q(n)
+                else:
+                    table(n)
+
+        def consume(item):
+            kind, n = item
+            if kind == "a":
+                squares(n)
+            elif kind == "x":
+                evac(n // 2, n % 2)
+            elif kind == "k":
+                rope_k(n)
+            elif kind == "q":
+                rope_q(n)
+            else:
+                base_t[n] = tabs.tile([P, CH, 2 * NPAIR], F32, name="base")
+                nc.scalar.copy(out=base_t[n][:], in_=tab_t[n][:])
+                qgain(2 * n, tab_t[n], nc.vector)
+                qgain(2 * n + 1, base_t[n], nc.gpsimd)
+
+        def swapped_weights():
+            pav = pa[:].rearrange("p (r u) (i e) -> p e r i u", u=2, e=2)
+            gqv = gwf[:, 0:256, :].rearrange("p (r i e) u -> p e r i u", r=2, e=2)
+            nc.vector.tensor_copy(out=gqv[:, 0], in_=pav[:, 1])
+            nc.vector.tensor_copy(out=gqv[:, 1], in_=pav[:, 0])
+            pbv = pb[:, :, 0:DH].rearrange("p u (i e) -> p e i u", e=2)
+            gkv = gwf[:, 512:576, :].rearrange("p (i e) u -> p e i u", e=2)
+            nc.vector.tensor_copy(out=gkv[:, 1], in_=pbv[:, 0])
+            pbb = pb[:].bitcast(BF16)[:, :, 0:2 * DH].rearrange("p u (i e f) -> p e i u f", e=2, f=2)
+            nc.vector.tensor_scalar(out=gwb[:, 0, 256:288], in0=pbb[:, 1], scalar1=-1.0, scalar2=None, op0=ALU.mult)
+            quant_w(0, 256)
+            quant_w(512, 576)
+
+        make("a", 2)
+        consume(a_items[0])
+        consume(a_items[1])
+        nc.scalar.activation(out=trig[:], in_=na[:], func=ACT.Sin, scale=-TWO_PI)
+        nc.scalar.activation(out=warm[:, 1:2], in_=ones[:], func=ACT.Abs_reciprocal_sqrt)
+        for c in range(NCH):
+            table_rows(c)
         quant_w(256, 512)
         quant_w(576, 704)
-        angles(0, 1)
         quant(0)
-        m1(0)
-        m1(1)
-        angles(1, NCH)
-        nc.scalar.activation(out=warm[:, 1:2], in_=ones[:], func=ACT.Abs_reciprocal_sqrt)
-
-        pav = pa[:].rearrange("p (r u) (i e) -> p e r i u", u=2, e=2)
-        gqv = gwf[:, 0:256, :].rearrange("p (r i e) u -> p e r i u", r=2, e=2)
-        nc.vector.tensor_copy(out=gqv[:, 0], in_=pav[:, 1])
-        nc.vector.tensor_copy(out=gqv[:, 1], in_=pav[:, 0])
-        pbv = pb[:, :, 0:DH].rearrange("p u (i e) -> p e i u", e=2)
-        gkv = gwf[:, 512:576, :].rearrange("p (i e) u -> p e i u", e=2)
-        nc.vector.tensor_copy(out=gkv[:, 1], in_=pbv[:, 0])
-        pbb = pb[:].bitcast(BF16)[:, :, 0:2 * DH].rearrange("p u (i e f) -> p e i u f", e=2, f=2)
-        nc.vector.tensor_scalar(out=gwb[:, 0, 256:288], in0=pbb[:, 1], scalar1=-1.0, scalar2=None, op0=ALU.mult)
-        quant_w(0, 256)
-        quant_w(512, 576)
-
-        pg = bank("q2", [P, 2 * DH])
+        make("a", 5)
+        pg = bank("d2", [P, 2 * DH])
         nc.tensor.matmul(out=pg[:], lhsT=ones_bf[:], rhs=gains[:], start=True, stop=True)
+        make("d", 1)
+        swapped_weights()
         gg = consts.tile([P, 2 * DH], F32, name="gg")
         gk = consts.tile([P, DH], F32, name="gk")
         nc.vector.tensor_copy(out=gg[:, DH:2 * DH], in_=pg[:, 0:DH])
@@ -386,64 +417,47 @@ def tile_attention_pa_t_kernel(tc, x, wq, wkv, q_norm_w, k_norm_w, out_0, out_1,
         nc.vector.tensor_scalar(out=ggs[:, 0], in0=pgs[:, 0], scalar1=-1.0, scalar2=None, op0=ALU.mult)
         nc.vector.tensor_copy(out=ggs[:, 1], in_=pgs[:, 1])
         nc.vector.tensor_copy(out=gk[:], in_=pg[:, DH:2 * DH])
-
-        transposes(1)
-        evac(1, 0)
-        evac(1, 1)
-        table(0)
+        consume(a_items[2])
+        evac(1, 0, on_vector=True)
+        make("a", 6)
+        consume(a_items[3])
+        make("a", 7)
+        evac(1, 1, on_vector=True)
+        consume(d_items[0])
+        make("d", 4)
         quant(1)
-        transposes(2)
-        for i in range(GR):
-            m1(i + D1)
-            squares(i)
-            if i < 2:
-                evac(2, i)
-            if i == 1:
-                qgain(0, tab_t[0])
-                qgain(1, base_t[0])
-        for j in range(D2):
-            m2q(j)
-        m2k(0)
+        make("a", 8)
+        for n in range(6, a_head):
+            consume(a_items[n])
+            make("a", n + 1 + PA)
+            if n == 7:
+                make("d", PD + 1)
 
-        for g in range(NG):
+        for v in range(NT):
+            g, i = divmod(v, GR)
             c, half = divmod(g, 2)
-            if g + 3 < NG:
-                transposes(g + 3)
-            rope_k(g)
-            for i in range(GR):
-                j = GR * g + i
-                s = j + GR
-                if i == 1 and g + 2 < NG:
-                    quant(g + 2)
-                if s + D1 < NT:
-                    m1(s + D1)
-                if i == 1 and g + 1 < NG:
-                    m2k(g + 1)
-                if j + D2 < NT:
-                    m2q(j + D2)
-                if s < NT:
-                    squares(s)
-                if g + 3 < NG and i < 2:
-                    evac(g + 3, i)
-                rope_q(j)
-                if i == 1 and half == 0 and c + 1 < NCH:
-                    table(c + 1)
-                if i == 3 and c + 1 < NCH:
-                    if half == 0:
-                        qgain(g + 2, tab_t[c + 1])
-                    else:
-                        qgain(g + 2, base_t[c + 1])
-                if g == NG - 1 and i == 1:
-                    add_q(nc.gpsimd, g, 0, 2)
-                    add_k(g)
-                    store_q(c, 0, GR + 2)
-                    store_k(c)
-            if g == NG - 1:
-                add_q(nc.vector, g, 2, GR)
-                store_q(c, GR + 2, CH)
-            else:
-                add_q(nc.vector if g in VECTOR_ADDS else nc.gpsimd, g, 0, GR)
+            for n in range(*d_at[v]):
+                consume(d_items[n])
+                make("d", n + 1 + PD)
+            for n in range(*a_at[v]):
+                consume(a_items[n])
+            if v == 0:
+                quant(2)
+            if i == 1 and g + 3 < NG:
+                quant(g + 3)
+            make("a", a_at[v][1] + PA)
+            if i == 0:
                 add_k(g)
                 if half == 1:
-                    store_q(c, 0, CH)
                     store_k(c)
+            if g < NG - 1:
+                if i == GR - 1:
+                    add_q(nc.vector if g in VECTOR_ADDS else nc.gpsimd, g, 0, GR)
+                    if half == 1:
+                        store_q(c, 0, CH)
+            elif i == 1:
+                add_q(nc.gpsimd, g, 0, 2)
+                store_q(c, 0, GR + 2)
+            elif i == 3:
+                add_q(nc.vector, g, 2, GR)
+                store_q(c, GR + 2, CH)

@@ -29,7 +29,10 @@ NA = 3
 ND = 5
 PA = 3
 PD = 5
-TABV = 2
+TABV = 5
+QI = 3
+XO = 15
+FENCE = True
 EPS = 1.1920929e-07
 TWO_PI = 6.283185307179586
 WCOLS = 704
@@ -91,10 +94,11 @@ def tile_attention_pa_t_kernel(tc, x, wq, wkv, q_norm_w, k_norm_w, out_0, out_1,
         make_identity(nc, ident[:])
         kpi = consts.tile([P, 1], I32, name="kpi")
         nc.gpsimd.iota(kpi[:], pattern=[[0, 1]], base=0, channel_multiplier=1)
-        NPOS = P + 2 * NT
+        NPOS = P + 3 * CH
         posi = consts.tile([P, NPOS], I32, name="posi")
         nc.gpsimd.iota(posi[:, 0:P], pattern=[[NT, P]], base=0, channel_multiplier=0)
-        nc.gpsimd.iota(posi[:, P:NPOS], pattern=[[1, NT], [0, 2]], base=0, channel_multiplier=0)
+        nc.gpsimd.iota(posi[:, P:P + 2 * CH], pattern=[[1, CH], [0, 2]], base=0, channel_multiplier=0)
+        nc.gpsimd.iota(posi[:, P + 2 * CH:NPOS], pattern=[[CH, CH]], base=0, channel_multiplier=0)
         ones = consts.tile([P, 1], F32, name="ones")
         eps_t = consts.tile([P, 1], F32, name="eps_t")
         ones_bf = consts.tile([P, P], BF16, name="ones_bf")
@@ -119,8 +123,15 @@ def tile_attention_pa_t_kernel(tc, x, wq, wkv, q_norm_w, k_norm_w, out_0, out_1,
         fk = consts.tile([P, 2], F32, name="fk")
         un = consts.tile([P, NPOS], F32, name="un")
         ki = consts.tile([P, NPOS], I32, name="ki")
-        na = consts.tile([P, NPOS], F32, name="na")
-        trig = consts.tile([P, NPOS], F32, name="trig")
+        NA_W = P + 2 * CH
+        na = consts.tile([P, NA_W], F32, name="na")
+        nb = consts.tile([P, CH], F32, name="nb")
+        nb1 = consts.tile([P, CH], F32, name="nb1")
+        vr = consts.tile([P, 2 * CH], F32, name="vr")
+        nv = consts.tile([P, CH, P], F32, name="nv")
+        nv2 = consts.tile([P, CH, P], F32, name="nv2")
+        ac = consts.tile([P, CH, P], F32, name="ac")
+        CC = slice(P + 2 * CH, NPOS)
         nc.vector.tensor_copy(out=kpf[:], in_=kpi[:])
         nc.vector.tensor_copy(out=posf[:], in_=posi[:])
         nc.vector.tensor_scalar(out=s4[:], in0=kpf[:], scalar1=float(NPAIR), scalar2=0.25, op0=ALU.is_ge, op1=ALU.mult)
@@ -130,14 +141,18 @@ def tile_attention_pa_t_kernel(tc, x, wq, wkv, q_norm_w, k_norm_w, out_0, out_1,
         nc.vector.tensor_tensor(out=fsel[:], in0=frow[:], in1=mask[:].unsqueeze(1).to_broadcast([P, 2, NPAIR]),
                                 op=ALU.mult)
         nc.vector.tensor_reduce(out=fk[:], in_=fsel[:], op=ALU.add, axis=AX.X)
-        por = posf[:, P:NPOS].rearrange("p (r c) -> p c r", c=2)
+        por = posf[:, P:NA_W].rearrange("p (r c) -> p c r", c=2)
         for dst in (ki, un):
-            dsr = dst[:, P:NPOS].rearrange("p (r c) -> p c r", c=2)
+            dsr = dst[:, P:NA_W].rearrange("p (r c) -> p c r", c=2)
+            nc.vector.tensor_scalar(out=dst[:, CC], in0=posf[:, CC], scalar1=fk[:, 0:1], scalar2=None, op0=ALU.mult)
             for o, src, phase in ((dst[:, 0:P], posf[:, 0:P], php), (dsr[:, 0], por[:, 0], s4), (dsr[:, 1], por[:, 1], phr)):
                 nc.vector.tensor_scalar(out=o, in0=src, scalar1=fk[:, 0:1], scalar2=phase[:], op0=ALU.mult, op1=ALU.add)
         nc.vector.tensor_tensor(out=un[:], in0=un[:], in1=ki[:], op=ALU.subtract)
         nc.vector.scalar_tensor_tensor(out=un[:], in0=posf[:], scalar=fk[:, 1:2], in1=un[:], op0=ALU.mult, op1=ALU.add)
-        nc.vector.scalar_tensor_tensor(out=na[:], in0=un[:], scalar=0.5, in1=un[:], op0=ALU.is_ge, op1=ALU.subtract)
+        nc.vector.scalar_tensor_tensor(out=na[:], in0=un[:, 0:NA_W], scalar=0.5, in1=un[:, 0:NA_W], op0=ALU.is_ge,
+                                       op1=ALU.subtract)
+        nc.vector.scalar_tensor_tensor(out=nb1[:], in0=un[:, CC], scalar=0.0, in1=un[:, CC], op0=ALU.is_lt, op1=ALU.add)
+        nc.vector.scalar_tensor_tensor(out=nb[:], in0=nb1[:], scalar=1.0, in1=nb1[:], op0=ALU.is_ge, op1=ALU.subtract)
 
         w32 = w_sb[:].bitcast(F32)
         gw = consts.tile([P, WCOLS * 4], BF16, name="gw", align_bytes=64)
@@ -208,19 +223,23 @@ def tile_attention_pa_t_kernel(tc, x, wq, wkv, q_norm_w, k_norm_w, out_0, out_1,
             xs_t[g] = codes.tile([P, GR * P], U8, name="xs", align_bytes=64)
             nc.vector.quantize_mx(out=xc_t[g][:].bitcast(FP8X4), scales=xs_t[g][:], in_=grp[g][:])
 
-        brow_t = {}
+        brow = consts.tile([P, CH * 2 * NPAIR], F32, name="brow")
 
-        def table_rows(c):
-            brow_t[c] = tabs.tile([P, CH * 2 * NPAIR], F32, name="brow", bufs=NCH)
-            cols = slice(P + 2 * CH * c, P + 2 * CH * c + 2 * CH)
-            nc.gpsimd.tensor_tensor(out=brow_t[c][:].rearrange("p (m i) -> p m i", i=NPAIR),
-                                    in0=trig[:, cols].unsqueeze(2).to_broadcast([P, 2 * CH, NPAIR]),
-                                    in1=mask[:].unsqueeze(1).to_broadcast([P, 2 * CH, NPAIR]), op=ALU.mult)
+        def flat(t, lo, hi):
+            return t[:, lo:hi, :].rearrange("p c n -> p (c n)")
+
+        def angles(lo, hi):
+            for c in range(lo, hi):
+                nc.vector.tensor_scalar(out=nv[:, c, :], in0=na[:, 0:P], scalar1=nb[:, c:c + 1], scalar2=None,
+                                        op0=ALU.add)
+            nc.vector.scalar_tensor_tensor(out=flat(nv2, lo, hi), in0=flat(nv, lo, hi), scalar=-0.5,
+                                           in1=flat(nv, lo, hi), op0=ALU.is_lt, op1=ALU.add)
+            nc.scalar.activation(out=flat(ac, lo, hi), in_=flat(nv2, lo, hi), func=ACT.Sin, scale=-TWO_PI)
 
         def table(c):
             tb = next_bank("d", [P, CH, 2 * NPAIR])
             tab_t[c] = tb
-            nc.tensor.matmul(out=tb[:].rearrange("p j m -> p (j m)"), lhsT=trig[:, 0:P], rhs=brow_t[c][:], start=True, stop=True)
+            nc.tensor.matmul(out=tb[:].rearrange("p j m -> p (j m)"), lhsT=ac[:, c, :], rhs=brow[:], start=True, stop=True)
 
         def qgain(g, src, eng):
             half = slice(GR * (g % 2), GR * (g % 2) + GR)
@@ -337,7 +356,7 @@ def tile_attention_pa_t_kernel(tc, x, wq, wkv, q_norm_w, k_norm_w, out_0, out_1,
             n0, m0 = len(a_items), len(d_items)
             if v + LS < NT:
                 a_items.append(("a", v + LS))
-            xg, xr = divmod(v + 15, GR)
+            xg, xr = divmod(v + XO, GR)
             if xr % 2 == 0 and xg < NG:
                 a_items.append(("x", 2 * xg + xr // 2))
             if v % GR == 0:
@@ -379,7 +398,7 @@ def tile_attention_pa_t_kernel(tc, x, wq, wkv, q_norm_w, k_norm_w, out_0, out_1,
                 base_t[n] = tabs.tile([P, CH, 2 * NPAIR], F32, name="base")
                 nc.scalar.copy(out=base_t[n][:], in_=tab_t[n][:])
                 qgain(2 * n, tab_t[n], nc.vector)
-                qgain(2 * n + 1, base_t[n], nc.gpsimd)
+                qgain(2 * n + 1, tab_t[n], nc.vector)
 
         def swapped_weights():
             pav = pa[:].rearrange("p (r u) (i e) -> p e r i u", u=2, e=2)
@@ -397,17 +416,27 @@ def tile_attention_pa_t_kernel(tc, x, wq, wkv, q_norm_w, k_norm_w, out_0, out_1,
         make("a", 2)
         consume(a_items[0])
         consume(a_items[1])
-        nc.scalar.activation(out=trig[:], in_=na[:], func=ACT.Sin, scale=-TWO_PI)
-        nc.scalar.activation(out=warm[:, 1:2], in_=ones[:], func=ACT.Abs_reciprocal_sqrt)
-        for c in range(NCH):
-            table_rows(c)
+        nc.scalar.activation(out=vr[:], in_=na[:, P:NA_W], func=ACT.Sin, scale=-TWO_PI)
         quant_w(256, 512)
         quant_w(576, 704)
         quant(0)
         make("a", 5)
+        consume(a_items[2])
+        make("a", 6)
+        consume(a_items[3])
+        angles(0, NCH)
+        nc.scalar.activation(out=warm[:, 1:2], in_=ones[:], func=ACT.Abs_reciprocal_sqrt)
+        evac(1, 0, on_vector=True)
+        nc.vector.tensor_tensor(out=brow[:].rearrange("p (m i) -> p m i", i=NPAIR),
+                                in0=vr[:].unsqueeze(2).to_broadcast([P, 2 * CH, NPAIR]),
+                                in1=mask[:].unsqueeze(1).to_broadcast([P, 2 * CH, NPAIR]), op=ALU.mult)
+        make("a", 8)
         pg = bank("d2", [P, 2 * DH])
         nc.tensor.matmul(out=pg[:], lhsT=ones_bf[:], rhs=gains[:], start=True, stop=True)
         make("d", 1)
+        evac(1, 1, on_vector=True)
+        consume(a_items[6])
+        consume(a_items[7])
         swapped_weights()
         gg = consts.tile([P, 2 * DH], F32, name="gg")
         gk = consts.tile([P, DH], F32, name="gk")
@@ -417,22 +446,18 @@ def tile_attention_pa_t_kernel(tc, x, wq, wkv, q_norm_w, k_norm_w, out_0, out_1,
         nc.vector.tensor_scalar(out=ggs[:, 0], in0=pgs[:, 0], scalar1=-1.0, scalar2=None, op0=ALU.mult)
         nc.vector.tensor_copy(out=ggs[:, 1], in_=pgs[:, 1])
         nc.vector.tensor_copy(out=gk[:], in_=pg[:, DH:2 * DH])
-        consume(a_items[2])
-        evac(1, 0, on_vector=True)
-        make("a", 6)
-        consume(a_items[3])
-        make("a", 7)
-        evac(1, 1, on_vector=True)
-        consume(d_items[0])
         make("d", 4)
         quant(1)
-        make("a", 8)
-        for n in range(6, a_head):
+        make("a", 11)
+        make("d", PD)
+        consume(d_items[0])
+        make("d", PD + 1)
+        for n in range(8, a_head):
+            make("a", n + PA)
             consume(a_items[n])
-            make("a", n + 1 + PA)
-            if n == 7:
-                make("d", PD + 1)
+        make("a", a_head + PA)
 
+        fence = consts.tile([P, NG], U32, name="fence")
         for v in range(NT):
             g, i = divmod(v, GR)
             c, half = divmod(g, 2)
@@ -443,8 +468,10 @@ def tile_attention_pa_t_kernel(tc, x, wq, wkv, q_norm_w, k_norm_w, out_0, out_1,
                 consume(a_items[n])
             if v == 0:
                 quant(2)
-            if i == 1 and g + 3 < NG:
+            if i == QI and g + 3 < NG:
                 quant(g + 3)
+                if FENCE:
+                    nc.gpsimd.tensor_copy(out=fence[:, g:g + 1], in_=xc_t[g + 3][:, 0:1])
             make("a", a_at[v][1] + PA)
             if i == 0:
                 add_k(g)

@@ -28,15 +28,16 @@ LS = 6
 NA = 3
 ND = 5
 PA = 3
-PD = 5
+PD = 4
 TABV = 5
+BASEV = 4
 QI = 3
 XO = 15
 FENCE = True
 EPS = 1.1920929e-07
 TWO_PI = 6.283185307179586
 WCOLS = 704
-VECTOR_ADDS = (NG - 1,)
+VECTOR_ADDS = (NG - 2,)
 
 
 def turn_constants():
@@ -395,10 +396,12 @@ def tile_attention_pa_t_kernel(tc, x, wq, wkv, q_norm_w, k_norm_w, out_0, out_1,
             elif kind == "q":
                 rope_q(n)
             else:
-                base_t[n] = tabs.tile([P, CH, 2 * NPAIR], F32, name="base")
-                nc.scalar.copy(out=base_t[n][:], in_=tab_t[n][:])
                 qgain(2 * n, tab_t[n], nc.vector)
                 qgain(2 * n + 1, tab_t[n], nc.vector)
+
+        def copy_base(c):
+            base_t[c] = tabs.tile([P, CH, 2 * NPAIR], F32, name="base")
+            nc.scalar.copy(out=base_t[c][:], in_=tab_t[c][:])
 
         def swapped_weights():
             pav = pa[:].rearrange("p (r u) (i e) -> p e r i u", u=2, e=2)
@@ -450,6 +453,7 @@ def tile_attention_pa_t_kernel(tc, x, wq, wkv, q_norm_w, k_norm_w, out_0, out_1,
         quant(1)
         make("a", 11)
         make("d", PD)
+        copy_base(0)
         consume(d_items[0])
         make("d", PD + 1)
         for n in range(8, a_head):
@@ -466,6 +470,8 @@ def tile_attention_pa_t_kernel(tc, x, wq, wkv, q_norm_w, k_norm_w, out_0, out_1,
                 make("d", n + 1 + PD)
             for n in range(*a_at[v]):
                 consume(a_items[n])
+            if v % CH == BASEV and v // CH + 1 < NCH:
+                copy_base(v // CH + 1)
             if v == 0:
                 quant(2)
             if i == QI and g + 3 < NG:
@@ -482,9 +488,9 @@ def tile_attention_pa_t_kernel(tc, x, wq, wkv, q_norm_w, k_norm_w, out_0, out_1,
                     add_q(nc.vector if g in VECTOR_ADDS else nc.gpsimd, g, 0, GR)
                     if half == 1:
                         store_q(c, 0, CH)
-            elif i == 1:
-                add_q(nc.gpsimd, g, 0, 2)
-                store_q(c, 0, GR + 2)
+            elif i == 0:
+                add_q(nc.gpsimd, g, 0, 1)
+                store_q(c, 0, GR + 1)
             elif i == 3:
-                add_q(nc.vector, g, 2, GR)
-                store_q(c, GR + 2, CH)
+                add_q(nc.vector, g, 1, GR)
+                store_q(c, GR + 1, CH)

@@ -30,6 +30,9 @@ ND = 5
 PA = 3
 PD = 4
 TABV = 5
+RSI = 0
+BASE_V = True
+EVV = 0
 BASEV = 4
 QI = 3
 XO = 15
@@ -120,6 +123,7 @@ def tile_attention_pa_t_kernel(tc, x, wq, wkv, q_norm_w, k_norm_w, out_0, out_1,
         phr = consts.tile([P, 1], F32, name="phr")
         posf = consts.tile([P, NPOS], F32, name="posf")
         mask = consts.tile([P, NPAIR], F32, name="mask")
+        perm = consts.tile([P, P], F32, name="perm")
         fsel = consts.tile([P, 2, NPAIR], F32, name="fsel")
         fk = consts.tile([P, 2], F32, name="fk")
         un = consts.tile([P, NPOS], F32, name="un")
@@ -133,6 +137,10 @@ def tile_attention_pa_t_kernel(tc, x, wq, wkv, q_norm_w, k_norm_w, out_0, out_1,
         nv2 = consts.tile([P, CH, P], F32, name="nv2")
         ac = consts.tile([P, CH, P], F32, name="ac")
         CC = slice(P + 2 * CH, NPOS)
+        idv = ident[:].rearrange("p (i e) -> p e i", e=2)
+        pmv = perm[:].rearrange("p (i e) -> p e i", e=2)
+        nc.vector.tensor_copy(out=pmv[:, 0], in_=idv[:, 1])
+        nc.vector.tensor_copy(out=pmv[:, 1], in_=idv[:, 0])
         nc.vector.tensor_copy(out=kpf[:], in_=kpi[:])
         nc.vector.tensor_copy(out=posf[:], in_=posi[:])
         nc.vector.tensor_scalar(out=s4[:], in0=kpf[:], scalar1=float(NPAIR), scalar2=0.25, op0=ALU.is_ge, op1=ALU.mult)
@@ -162,21 +170,21 @@ def tile_attention_pa_t_kernel(tc, x, wq, wkv, q_norm_w, k_norm_w, out_0, out_1,
         gwf = gw[:].bitcast(F32).rearrange("p (c u) -> p c u", u=2)
         gwb = gw[:].rearrange("p (i e u f) -> p e i u f", e=2, u=2, f=2)
 
-        def w_transposes(dst, slot, r):
+        def w_transposes(dst, slot, r, mat):
             for u in range(2):
-                nc.tensor.transpose(dst[:, slot + u, :], w32[:, r, u:2 * P:2], ident[:])
+                nc.tensor.transpose(dst[:, slot + u, :], w32[:, r, u:2 * P:2], mat[:])
 
         def quant_w(lo, hi):
             nc.vector.quantize_mx(out=wc[:, lo:hi].bitcast(FP8X4), scales=ws[:, lo:hi], in_=gw[:, 4 * lo:4 * hi])
 
         pa = bank("d4", [P, 4, P])
-        w_transposes(pa, 0, 0)
-        w_transposes(pa, 2, 1)
-        pb = bank("d3", [P, 2, P])
-        w_transposes(pb, 0, 2)
+        w_transposes(pa, 0, 0, ident)
+        w_transposes(pa, 2, 1, ident)
+        pb = bank("d3", [P, 4, P])
+        w_transposes(pb, 0, 2, ident)
         nc.scalar.copy(out=gwf[:, 256:512, :].rearrange("p (r c) u -> p r c u", r=2),
                        in_=pa[:].rearrange("p (r u) c -> p r c u", u=2))
-        nc.scalar.copy(out=gwf[:, 576:704, :], in_=pb[:].rearrange("p u c -> p c u"))
+        nc.scalar.copy(out=gwf[:, 576:704, :], in_=pb[:, 0:2, :].rearrange("p u c -> p c u"))
 
         grp = {}
         xc_t = {}
@@ -278,10 +286,12 @@ def tile_attention_pa_t_kernel(tc, x, wq, wkv, q_norm_w, k_norm_w, out_0, out_1,
                 nc.scalar.activation(out=junk[:, h, :], in_=ps[:, h * DH:(h + 1) * DH], func=ACT.Square,
                                      accum_out=ss_t[g][:, i * 5 + h:i * 5 + h + 1])
             nc.scalar.copy(out=ov_t[c][:, jj, :], in_=ps[:, 320:384])
-            if i == GR - 1:
-                rs_t[g] = small.tile([P, 5 * GR], F32, name="rs")
-                nc.scalar.activation(out=rs_t[g][:], in_=ss_t[g][:], func=ACT.Abs_reciprocal_sqrt, scale=1.0 / DH,
-                                     bias=eps_t[:])
+            if j == GR - 1 or (i == RSI and g > 1) or j == NT - 1:
+                q = g if j == GR - 1 or j == NT - 1 else g - 1
+                if True:
+                    rs_t[q] = small.tile([P, 5 * GR], F32, name="rs")
+                    nc.scalar.activation(out=rs_t[q][:], in_=ss_t[q][:], func=ACT.Abs_reciprocal_sqrt, scale=1.0 / DH,
+                                         bias=eps_t[:])
             if jj == CH - 1:
                 nc.sync.dma_start(out=ovv[:, c * CH:(c + 1) * CH, :], in_=ov_t[c][:])
 
@@ -390,33 +400,40 @@ def tile_attention_pa_t_kernel(tc, x, wq, wkv, q_norm_w, k_norm_w, out_0, out_1,
             if kind == "a":
                 squares(n)
             elif kind == "x":
-                evac(n // 2, n % 2)
+                evac(n // 2, n % 2, on_vector=n % 4 < EVV and n > 7)
             elif kind == "k":
                 rope_k(n)
             elif kind == "q":
                 rope_q(n)
             else:
+                if BASE_V:
+                    copy_base(n)
                 qgain(2 * n, tab_t[n], nc.vector)
                 qgain(2 * n + 1, tab_t[n], nc.vector)
 
         def copy_base(c):
             base_t[c] = tabs.tile([P, CH, 2 * NPAIR], F32, name="base")
-            nc.scalar.copy(out=base_t[c][:], in_=tab_t[c][:])
+            if BASE_V:
+                nc.vector.tensor_copy(out=base_t[c][:], in_=tab_t[c][:])
+            else:
+                nc.scalar.copy(out=base_t[c][:], in_=tab_t[c][:])
 
         def swapped_weights():
-            pav = pa[:].rearrange("p (r u) (i e) -> p e r i u", u=2, e=2)
-            gqv = gwf[:, 0:256, :].rearrange("p (r i e) u -> p e r i u", r=2, e=2)
-            nc.vector.tensor_copy(out=gqv[:, 0], in_=pav[:, 1])
-            nc.vector.tensor_copy(out=gqv[:, 1], in_=pav[:, 0])
-            pbv = pb[:, :, 0:DH].rearrange("p u (i e) -> p e i u", e=2)
+            nc.vector.tensor_copy(out=gwf[:, 0:256, :].rearrange("p (r c) u -> p r c u", r=2),
+                                  in_=pc[:].rearrange("p (r u) c -> p r c u", u=2))
+            pbv = pb[:, 2:4, 0:DH].rearrange("p u (i e) -> p e i u", e=2)
             gkv = gwf[:, 512:576, :].rearrange("p (i e) u -> p e i u", e=2)
-            nc.vector.tensor_copy(out=gkv[:, 1], in_=pbv[:, 0])
-            pbb = pb[:].bitcast(BF16)[:, :, 0:2 * DH].rearrange("p u (i e f) -> p e i u f", e=2, f=2)
-            nc.vector.tensor_scalar(out=gwb[:, 0, 256:288], in0=pbb[:, 1], scalar1=-1.0, scalar2=None, op0=ALU.mult)
+            nc.vector.tensor_copy(out=gkv[:, 1], in_=pbv[:, 1])
+            pbb = pb[:].bitcast(BF16)[:, 2:4, 0:2 * DH].rearrange("p u (i e f) -> p e i u f", e=2, f=2)
+            nc.vector.tensor_scalar(out=gwb[:, 0, 256:288], in0=pbb[:, 0], scalar1=-1.0, scalar2=None, op0=ALU.mult)
             quant_w(0, 256)
             quant_w(512, 576)
 
         make("a", 2)
+        w_transposes(pb, 2, 2, perm)
+        pc = bank("d2", [P, 4, P])
+        w_transposes(pc, 0, 0, perm)
+        w_transposes(pc, 2, 1, perm)
         consume(a_items[0])
         consume(a_items[1])
         nc.scalar.activation(out=vr[:], in_=na[:, P:NA_W], func=ACT.Sin, scale=-TWO_PI)
@@ -434,7 +451,7 @@ def tile_attention_pa_t_kernel(tc, x, wq, wkv, q_norm_w, k_norm_w, out_0, out_1,
                                 in0=vr[:].unsqueeze(2).to_broadcast([P, 2 * CH, NPAIR]),
                                 in1=mask[:].unsqueeze(1).to_broadcast([P, 2 * CH, NPAIR]), op=ALU.mult)
         make("a", 8)
-        pg = bank("d2", [P, 2 * DH])
+        pg = bank("d1", [P, 2 * DH])
         nc.tensor.matmul(out=pg[:], lhsT=ones_bf[:], rhs=gains[:], start=True, stop=True)
         make("d", 1)
         evac(1, 1, on_vector=True)
@@ -453,7 +470,8 @@ def tile_attention_pa_t_kernel(tc, x, wq, wkv, q_norm_w, k_norm_w, out_0, out_1,
         quant(1)
         make("a", 11)
         make("d", PD)
-        copy_base(0)
+        if not BASE_V:
+            copy_base(0)
         consume(d_items[0])
         make("d", PD + 1)
         for n in range(8, a_head):
@@ -470,7 +488,7 @@ def tile_attention_pa_t_kernel(tc, x, wq, wkv, q_norm_w, k_norm_w, out_0, out_1,
                 make("d", n + 1 + PD)
             for n in range(*a_at[v]):
                 consume(a_items[n])
-            if v % CH == BASEV and v // CH + 1 < NCH:
+            if v % CH == BASEV and v // CH + 1 < NCH and not BASE_V:
                 copy_base(v // CH + 1)
             if v == 0:
                 quant(2)

@@ -31,11 +31,13 @@ PA = 3
 PD = 4
 TABV = 5
 RSI = 0
-BASE_V = True
+BASE_V = False
 EVV = 0
-BASEV = 4
+BASEV = 5
 QI = 3
 XO = 15
+KRI = 2
+XR = (0, 2)
 FENCE = True
 EPS = 1.1920929e-07
 TWO_PI = 6.283185307179586
@@ -203,6 +205,7 @@ def tile_attention_pa_t_kernel(tc, x, wq, wkv, q_norm_w, k_norm_w, out_0, out_1,
         pq_t = {}
         pk_t = {}
         xt_t = {}
+        kr_t = {}
         turn = {"a": 0, "d": 0}
 
         def next_bank(ring, shape):
@@ -237,12 +240,15 @@ def tile_attention_pa_t_kernel(tc, x, wq, wkv, q_norm_w, k_norm_w, out_0, out_1,
         def flat(t, lo, hi):
             return t[:, lo:hi, :].rearrange("p c n -> p (c n)")
 
-        def angles(lo, hi):
+        def angle_sums(lo, hi):
             for c in range(lo, hi):
-                nc.vector.tensor_scalar(out=nv[:, c, :], in0=na[:, 0:P], scalar1=nb[:, c:c + 1], scalar2=None,
-                                        op0=ALU.add)
+                nc.scalar.activation(out=nv[:, c, :], in_=na[:, 0:P], func=ACT.Identity, bias=nb[:, c:c + 1])
+
+        def wraps(lo, hi):
             nc.vector.scalar_tensor_tensor(out=flat(nv2, lo, hi), in0=flat(nv, lo, hi), scalar=-0.5,
                                            in1=flat(nv, lo, hi), op0=ALU.is_lt, op1=ALU.add)
+
+        def sines(lo, hi):
             nc.scalar.activation(out=flat(ac, lo, hi), in_=flat(nv2, lo, hi), func=ACT.Sin, scale=-TWO_PI)
 
         def table(c):
@@ -273,6 +279,13 @@ def tile_attention_pa_t_kernel(tc, x, wq, wkv, q_norm_w, k_norm_w, out_0, out_1,
             nc.tensor.matmul_mx(out=ps[:, 256:384], lhsT=lhs, lhsT_scale=lsc, rhs=wc[:, 576:704].bitcast(FP8X4),
                                 rhs_scale=ws[:, 576:704], start=True, stop=True)
 
+        def roots(g, lo, hi):
+            if lo == 0:
+                rs_t[g] = small.tile([P, 5 * GR], F32, name="rs")
+            cols = slice(5 * lo, 5 * hi)
+            nc.scalar.activation(out=rs_t[g][:, cols], in_=ss_t[g][:, cols], func=ACT.Abs_reciprocal_sqrt,
+                                 scale=1.0 / DH, bias=eps_t[:])
+
         def squares(j):
             g, i = divmod(j, GR)
             c, jj = divmod(j, CH)
@@ -286,12 +299,16 @@ def tile_attention_pa_t_kernel(tc, x, wq, wkv, q_norm_w, k_norm_w, out_0, out_1,
                 nc.scalar.activation(out=junk[:, h, :], in_=ps[:, h * DH:(h + 1) * DH], func=ACT.Square,
                                      accum_out=ss_t[g][:, i * 5 + h:i * 5 + h + 1])
             nc.scalar.copy(out=ov_t[c][:, jj, :], in_=ps[:, 320:384])
-            if j == GR - 1 or (i == RSI and g > 1) or j == NT - 1:
-                q = g if j == GR - 1 or j == NT - 1 else g - 1
-                if True:
-                    rs_t[q] = small.tile([P, 5 * GR], F32, name="rs")
-                    nc.scalar.activation(out=rs_t[q][:], in_=ss_t[q][:], func=ACT.Abs_reciprocal_sqrt, scale=1.0 / DH,
-                                         bias=eps_t[:])
+            if j == GR - 1:
+                roots(0, 2, GR)
+            elif i == RSI and g > 1:
+                roots(g - 1, 0, GR)
+            elif j == NT - 1:
+                roots(g, 0, GR)
+            if j >= GR and i == KRI:
+                k_factors(g - 1)
+            if j == NT - 1:
+                k_factors(g)
             if jj == CH - 1:
                 nc.sync.dma_start(out=ovv[:, c * CH:(c + 1) * CH, :], in_=ov_t[c][:])
 
@@ -313,12 +330,17 @@ def tile_attention_pa_t_kernel(tc, x, wq, wkv, q_norm_w, k_norm_w, out_0, out_1,
         def rope_k(g):
             c, half = divmod(g, 2)
             tk_t[g] = work.tile([P, GR, 2 * DH], F32, name="tk")
+            nc.vector.tensor_tensor(
+                out=tk_t[g][:].rearrange("p j (m e) -> p (j m) e", e=2),
+                in0=pk_t[g][:].rearrange("p j (m e) -> p (j m) e", e=2),
+                in1=base_t[c][:, half * GR:half * GR + GR, :].rearrange("p j m -> p (j m)").unsqueeze(2).to_broadcast(
+                    [P, GR * 2 * NPAIR, 2]), op=ALU.mult)
+
+        def k_factors(g):
+            kr_t[g] = work.tile([P, GR, DH], F32, name="kr")
             for i in range(GR):
-                nc.vector.scalar_tensor_tensor(
-                    out=tk_t[g][:, i, :].rearrange("p (m e) -> p m e", e=2),
-                    in0=pk_t[g][:, i, :].rearrange("p (m e) -> p m e", e=2), scalar=rs_t[g][:, i * 5 + 4:i * 5 + 5],
-                    in1=base_t[c][:, half * GR + i, :].unsqueeze(2).to_broadcast([P, 2 * NPAIR, 2]), op0=ALU.mult,
-                    op1=ALU.mult)
+                nc.scalar.activation(out=kr_t[g][:, i, :], in_=gk[:], func=ACT.Copy,
+                                     scale=rs_t[g][:, i * 5 + 4:i * 5 + 5])
 
         def rope_q(j):
             g, i = divmod(j, GR)
@@ -348,7 +370,7 @@ def tile_attention_pa_t_kernel(tc, x, wq, wkv, q_norm_w, k_norm_w, out_0, out_1,
             uk = work.tile([P, GR, DH], F32, name="uk")
             nc.gpsimd.tensor_tensor(out=uk[:], in0=tk_t[g][:, :, 0:DH], in1=tk_t[g][:, :, DH:2 * DH], op=ALU.add)
             nc.gpsimd.tensor_tensor(out=ok_t[c][:, half * GR:half * GR + GR, :], in0=uk[:],
-                                    in1=gk[:].unsqueeze(1).to_broadcast([P, GR, DH]), op=ALU.mult)
+                                    in1=kr_t[g][:], op=ALU.mult)
 
         def store_q(c, lo, hi):
             js = slice(c * CH + lo, c * CH + hi)
@@ -368,8 +390,9 @@ def tile_attention_pa_t_kernel(tc, x, wq, wkv, q_norm_w, k_norm_w, out_0, out_1,
             if v + LS < NT:
                 a_items.append(("a", v + LS))
             xg, xr = divmod(v + XO, GR)
-            if xr % 2 == 0 and xg < NG:
-                a_items.append(("x", 2 * xg + xr // 2))
+            for half in range(2):
+                if xr == XR[half] and xg < NG:
+                    a_items.append(("x", 2 * xg + half))
             if v % GR == 0:
                 d_items.append(("k", v // GR))
             d_items.append(("q", v))
@@ -406,28 +429,17 @@ def tile_attention_pa_t_kernel(tc, x, wq, wkv, q_norm_w, k_norm_w, out_0, out_1,
             elif kind == "q":
                 rope_q(n)
             else:
-                if BASE_V:
+                if BASE_V or n == 0:
                     copy_base(n)
                 qgain(2 * n, tab_t[n], nc.vector)
                 qgain(2 * n + 1, tab_t[n], nc.vector)
 
         def copy_base(c):
             base_t[c] = tabs.tile([P, CH, 2 * NPAIR], F32, name="base")
-            if BASE_V:
+            if BASE_V or c == 0:
                 nc.vector.tensor_copy(out=base_t[c][:], in_=tab_t[c][:])
             else:
                 nc.scalar.copy(out=base_t[c][:], in_=tab_t[c][:])
-
-        def swapped_weights():
-            nc.vector.tensor_copy(out=gwf[:, 0:256, :].rearrange("p (r c) u -> p r c u", r=2),
-                                  in_=pc[:].rearrange("p (r u) c -> p r c u", u=2))
-            pbv = pb[:, 2:4, 0:DH].rearrange("p u (i e) -> p e i u", e=2)
-            gkv = gwf[:, 512:576, :].rearrange("p (i e) u -> p e i u", e=2)
-            nc.vector.tensor_copy(out=gkv[:, 1], in_=pbv[:, 1])
-            pbb = pb[:].bitcast(BF16)[:, 2:4, 0:2 * DH].rearrange("p u (i e f) -> p e i u f", e=2, f=2)
-            nc.vector.tensor_scalar(out=gwb[:, 0, 256:288], in0=pbb[:, 0], scalar1=-1.0, scalar2=None, op0=ALU.mult)
-            quant_w(0, 256)
-            quant_w(512, 576)
 
         make("a", 2)
         w_transposes(pb, 2, 2, perm)
@@ -437,27 +449,33 @@ def tile_attention_pa_t_kernel(tc, x, wq, wkv, q_norm_w, k_norm_w, out_0, out_1,
         consume(a_items[0])
         consume(a_items[1])
         nc.scalar.activation(out=vr[:], in_=na[:, P:NA_W], func=ACT.Sin, scale=-TWO_PI)
+        angle_sums(0, NCH)
         quant_w(256, 512)
         quant_w(576, 704)
         quant(0)
         make("a", 5)
-        consume(a_items[2])
-        make("a", 6)
-        consume(a_items[3])
-        angles(0, NCH)
-        nc.scalar.activation(out=warm[:, 1:2], in_=ones[:], func=ACT.Abs_reciprocal_sqrt)
-        evac(1, 0, on_vector=True)
+        wraps(0, 1)
+        sines(0, 1)
         nc.vector.tensor_tensor(out=brow[:].rearrange("p (m i) -> p m i", i=NPAIR),
                                 in0=vr[:].unsqueeze(2).to_broadcast([P, 2 * CH, NPAIR]),
                                 in1=mask[:].unsqueeze(1).to_broadcast([P, 2 * CH, NPAIR]), op=ALU.mult)
-        make("a", 8)
+        wraps(1, NCH)
+        nc.scalar.copy(out=gwf[:, 0:256, :].rearrange("p (r c) u -> p r c u", r=2),
+                       in_=pc[:].rearrange("p (r u) c -> p r c u", u=2))
+        pbv = pb[:, 2:4, 0:DH].rearrange("p u (i e) -> p e i u", e=2)
+        gkv = gwf[:, 512:576, :].rearrange("p (i e) u -> p e i u", e=2)
+        nc.vector.tensor_copy(out=gkv[:, 1], in_=pbv[:, 1])
+        pbb = pb[:].bitcast(BF16)[:, 2:4, 0:2 * DH].rearrange("p u (i e f) -> p e i u f", e=2, f=2)
+        nc.vector.tensor_scalar(out=gwb[:, 0, 256:288], in0=pbb[:, 0], scalar1=-1.0, scalar2=None, op0=ALU.mult)
+        consume(a_items[2])
+        consume(a_items[3])
+        sines(1, NCH)
+        nc.scalar.activation(out=warm[:, 1:2], in_=ones[:], func=ACT.Abs_reciprocal_sqrt)
+        roots(0, 0, 2)
         pg = bank("d1", [P, 2 * DH])
         nc.tensor.matmul(out=pg[:], lhsT=ones_bf[:], rhs=gains[:], start=True, stop=True)
         make("d", 1)
-        evac(1, 1, on_vector=True)
-        consume(a_items[6])
-        consume(a_items[7])
-        swapped_weights()
+        make("a", 6)
         gg = consts.tile([P, 2 * DH], F32, name="gg")
         gk = consts.tile([P, DH], F32, name="gk")
         nc.vector.tensor_copy(out=gg[:, DH:2 * DH], in_=pg[:, 0:DH])
@@ -466,12 +484,16 @@ def tile_attention_pa_t_kernel(tc, x, wq, wkv, q_norm_w, k_norm_w, out_0, out_1,
         nc.vector.tensor_scalar(out=ggs[:, 0], in0=pgs[:, 0], scalar1=-1.0, scalar2=None, op0=ALU.mult)
         nc.vector.tensor_copy(out=ggs[:, 1], in_=pgs[:, 1])
         nc.vector.tensor_copy(out=gk[:], in_=pg[:, DH:2 * DH])
+        quant_w(0, 256)
+        quant_w(512, 576)
+        evac(1, 0, on_vector=True)
+        make("a", 8)
         make("d", 4)
+        evac(1, 1, on_vector=True)
+        consume(a_items[6])
+        consume(a_items[7])
         quant(1)
         make("a", 11)
-        make("d", PD)
-        if not BASE_V:
-            copy_base(0)
         consume(d_items[0])
         make("d", PD + 1)
         for n in range(8, a_head):
@@ -490,13 +512,13 @@ def tile_attention_pa_t_kernel(tc, x, wq, wkv, q_norm_w, k_norm_w, out_0, out_1,
                 consume(a_items[n])
             if v % CH == BASEV and v // CH + 1 < NCH and not BASE_V:
                 copy_base(v // CH + 1)
-            if v == 0:
+            if v == 1:
                 quant(2)
             if i == QI and g + 3 < NG:
                 quant(g + 3)
                 if FENCE:
                     nc.gpsimd.tensor_copy(out=fence[:, g:g + 1], in_=xc_t[g + 3][:, 0:1])
-            make("a", a_at[v][1] + PA)
+            make("a", a_at[v][1] + (PA if v > 0 else PA - 1))
             if i == 0:
                 add_k(g)
                 if half == 1:

@@ -25,8 +25,8 @@ NCH = 8
 GR = 4
 NG = 16
 LS = 6
-NA = 3
-ND = 5
+NA = 4
+ND = 4
 PA = 3
 PD = 4
 TABV = 5
@@ -36,8 +36,9 @@ EVV = 0
 BASEV = 5
 QI = 3
 XO = 15
+NX = 0
 KRI = 2
-XR = (0, 2)
+XR = (0, 0)
 FENCE = True
 EPS = 1.1920929e-07
 TWO_PI = 6.283185307179586
@@ -179,10 +180,10 @@ def tile_attention_pa_t_kernel(tc, x, wq, wkv, q_norm_w, k_norm_w, out_0, out_1,
         def quant_w(lo, hi):
             nc.vector.quantize_mx(out=wc[:, lo:hi].bitcast(FP8X4), scales=ws[:, lo:hi], in_=gw[:, 4 * lo:4 * hi])
 
-        pa = bank("d4", [P, 4, P])
+        pa = bank("d%d" % (ND - 1), [P, 4, P])
         w_transposes(pa, 0, 0, ident)
         w_transposes(pa, 2, 1, ident)
-        pb = bank("d3", [P, 4, P])
+        pb = bank("d%d" % (ND - 2), [P, 4, P])
         w_transposes(pb, 0, 2, ident)
         nc.scalar.copy(out=gwf[:, 256:512, :].rearrange("p (r c) u -> p r c u", r=2),
                        in_=pa[:].rearrange("p (r u) c -> p r c u", u=2))
@@ -206,15 +207,16 @@ def tile_attention_pa_t_kernel(tc, x, wq, wkv, q_norm_w, k_norm_w, out_0, out_1,
         pk_t = {}
         xt_t = {}
         kr_t = {}
-        turn = {"a": 0, "d": 0}
+        turn = {"a": 0, "d": 0, "x": 0}
+        depth = {"a": NA, "d": ND, "x": NX}
 
         def next_bank(ring, shape):
-            t = bank("%s%d" % (ring, turn[ring] % (NA if ring == "a" else ND)), shape)
+            t = bank("%s%d" % (ring, turn[ring] % depth[ring]), shape)
             turn[ring] += 1
             return t
 
         def transposes(g, b):
-            xt = next_bank("a", [P, 4, P])
+            xt = next_bank("x" if NX else "a", [P, 4, P])
             xt_t[2 * g + b] = xt
             for a in range(2):
                 for u in range(2):
@@ -390,9 +392,14 @@ def tile_attention_pa_t_kernel(tc, x, wq, wkv, q_norm_w, k_norm_w, out_0, out_1,
             if v + LS < NT:
                 a_items.append(("a", v + LS))
             xg, xr = divmod(v + XO, GR)
-            for half in range(2):
-                if xr == XR[half] and xg < NG:
-                    a_items.append(("x", 2 * xg + half))
+            if xg < NG:
+                if XR[0] == XR[1]:
+                    if xr == XR[0]:
+                        a_items.append(("xx", xg))
+                else:
+                    for half in range(2):
+                        if xr == XR[half]:
+                            a_items.append(("x", 2 * xg + half))
             if v % GR == 0:
                 d_items.append(("k", v // GR))
             d_items.append(("q", v))
@@ -411,6 +418,9 @@ def tile_attention_pa_t_kernel(tc, x, wq, wkv, q_norm_w, k_norm_w, out_0, out_1,
                     m1(n)
                 elif kind == "x":
                     transposes(n // 2, n % 2)
+                elif kind == "xx":
+                    transposes(n, 0)
+                    transposes(n, 1)
                 elif kind == "k":
                     m2k(n)
                 elif kind == "q":
@@ -423,7 +433,10 @@ def tile_attention_pa_t_kernel(tc, x, wq, wkv, q_norm_w, k_norm_w, out_0, out_1,
             if kind == "a":
                 squares(n)
             elif kind == "x":
-                evac(n // 2, n % 2, on_vector=n % 4 < EVV and n > 7)
+                evac(n // 2, n % 2)
+            elif kind == "xx":
+                evac(n, 0)
+                evac(n, 1)
             elif kind == "k":
                 rope_k(n)
             elif kind == "q":
@@ -443,7 +456,7 @@ def tile_attention_pa_t_kernel(tc, x, wq, wkv, q_norm_w, k_norm_w, out_0, out_1,
 
         make("a", 2)
         w_transposes(pb, 2, 2, perm)
-        pc = bank("d2", [P, 4, P])
+        pc = bank("d%d" % (ND - 3), [P, 4, P])
         w_transposes(pc, 0, 0, perm)
         w_transposes(pc, 2, 1, perm)
         consume(a_items[0])
@@ -472,7 +485,7 @@ def tile_attention_pa_t_kernel(tc, x, wq, wkv, q_norm_w, k_norm_w, out_0, out_1,
         sines(1, NCH)
         nc.scalar.activation(out=warm[:, 1:2], in_=ones[:], func=ACT.Abs_reciprocal_sqrt)
         roots(0, 0, 2)
-        pg = bank("d1", [P, 2 * DH])
+        pg = bank("d%d" % (ND - 2), [P, 2 * DH])
         nc.tensor.matmul(out=pg[:], lhsT=ones_bf[:], rhs=gains[:], start=True, stop=True)
         make("d", 1)
         make("a", 6)

@@ -36,10 +36,10 @@ EVV = 0
 BASEV = 5
 QI = 3
 XO = 15
+TS = 1
 NX = 0
 KRI = 2
 XR = (0, 0)
-FENCE = True
 EPS = 1.1920929e-07
 TWO_PI = 6.283185307179586
 WCOLS = 704
@@ -344,13 +344,13 @@ def tile_attention_pa_t_kernel(tc, x, wq, wkv, q_norm_w, k_norm_w, out_0, out_1,
                 nc.scalar.activation(out=kr_t[g][:, i, :], in_=gk[:], func=ACT.Copy,
                                      scale=rs_t[g][:, i * 5 + 4:i * 5 + 5])
 
-        def rope_q(j):
+        def rope_q(j, first=0, last=4):
             g, i = divmod(j, GR)
             if i == 0:
                 tq_t[g] = work.tile([P, GR, 512], F32, name="tq")
             pv = pq_t[j][:].rearrange("p (c h d) -> p h c d", c=2, h=4)
             tv = tq_t[g][:, i, :].rearrange("p (c h d) -> p h c d", c=2, h=4)
-            for h in range(4):
+            for h in range(first, last):
                 nc.vector.scalar_tensor_tensor(out=tv[:, h], in0=pv[:, h], scalar=rs_t[g][:, i * 5 + h:i * 5 + h + 1],
                                                in1=qtab_t[g][:, i, :].rearrange("p (c d) -> p c d", c=2), op0=ALU.mult,
                                                op1=ALU.mult)
@@ -440,7 +440,12 @@ def tile_attention_pa_t_kernel(tc, x, wq, wkv, q_norm_w, k_norm_w, out_0, out_1,
             elif kind == "k":
                 rope_k(n)
             elif kind == "q":
-                rope_q(n)
+                if n % GR == QI and n // GR + 3 < NG:
+                    rope_q(n, 0, 3)
+                    quant(n // GR + 3)
+                    rope_q(n, 3, 4)
+                else:
+                    rope_q(n)
             else:
                 if BASE_V or n == 0:
                     copy_base(n)
@@ -514,7 +519,6 @@ def tile_attention_pa_t_kernel(tc, x, wq, wkv, q_norm_w, k_norm_w, out_0, out_1,
             consume(a_items[n])
         make("a", a_head + PA)
 
-        fence = consts.tile([P, NG], U32, name="fence")
         for v in range(NT):
             g, i = divmod(v, GR)
             c, half = divmod(g, 2)
@@ -527,10 +531,6 @@ def tile_attention_pa_t_kernel(tc, x, wq, wkv, q_norm_w, k_norm_w, out_0, out_1,
                 copy_base(v // CH + 1)
             if v == 1:
                 quant(2)
-            if i == QI and g + 3 < NG:
-                quant(g + 3)
-                if FENCE:
-                    nc.gpsimd.tensor_copy(out=fence[:, g:g + 1], in_=xc_t[g + 3][:, 0:1])
             make("a", a_at[v][1] + (PA if v > 0 else PA - 1))
             if i == 0:
                 add_k(g)
@@ -541,9 +541,9 @@ def tile_attention_pa_t_kernel(tc, x, wq, wkv, q_norm_w, k_norm_w, out_0, out_1,
                     add_q(nc.vector if g in VECTOR_ADDS else nc.gpsimd, g, 0, GR)
                     if half == 1:
                         store_q(c, 0, CH)
-            elif i == 0:
-                add_q(nc.gpsimd, g, 0, 1)
-                store_q(c, 0, GR + 1)
+            elif i == TS - 1:
+                add_q(nc.gpsimd, g, 0, TS)
+                store_q(c, 0, GR + TS)
             elif i == 3:
-                add_q(nc.vector, g, 1, GR)
-                store_q(c, GR + 1, CH)
+                add_q(nc.vector, g, TS, GR)
+                store_q(c, GR + TS, CH)

from contextlib import ExitStack

import concourse.mybir as mybir
from concourse.masks import make_identity

FLOPS = 2 * 8192 * 512 * 384

F32 = mybir.dt.float32
BF16 = mybir.dt.bfloat16
I32 = mybir.dt.int32
U32 = mybir.dt.uint32
U8 = mybir.dt.uint8
FP8X4 = mybir.dt.float8_e4m3fn_x4
ALU = mybir.AluOpType
ACT = mybir.ActivationFunctionType
AX = mybir.AxisListType

P = 128
D = 512
DH = 64
NPAIR = 32
NT = 64
CH = 8
NCH = 8
GR = 4
NG = 16
LS = 6
NA = 4
ND = 4
PA = 3
PD = 4
TABV = 5
RSI = 0
BASE_V = False
EVV = 0
BASEV = 5
QI = 3
XO = 15
TS = 1
NX = 0
KRI = 2
XR = (0, 0)
EPS = 1.1920929e-07
TWO_PI = 6.283185307179586
WCOLS = 704
VECTOR_ADDS = (NG - 2,)


def turn_constants():
    his = []
    los = []
    for i in range(NPAIR):
        f = 10000.0 ** (-2.0 * i / DH) / TWO_PI
        e = 0
        while f * 2.0 ** e < 1.0:
            e += 1
        scale = 2.0 ** (e + 13)
        hi = int(f * scale) / scale
        his.append(hi)
        los.append(f - hi)
    return his, los


def tile_attention_pa_t_kernel(tc, x, wq, wkv, q_norm_w, k_norm_w, out_0, out_1, out_2):
    nc = tc.nc
    with ExitStack() as ctx:
        ctx.enter_context(tc.manual_schedule())
        consts = ctx.enter_context(tc.tile_pool(name="consts", bufs=1))
        xin = ctx.enter_context(tc.tile_pool(name="xin", bufs=NG))
        grps = ctx.enter_context(tc.tile_pool(name="grps", bufs=3))
        codes = ctx.enter_context(tc.tile_pool(name="codes", bufs=4))
        small = ctx.enter_context(tc.tile_pool(name="small", bufs=4))
        junks = ctx.enter_context(tc.tile_pool(name="junks", bufs=8))
        tabs = ctx.enter_context(tc.tile_pool(name="tabs", bufs=3))
        work = ctx.enter_context(tc.tile_pool(name="work", bufs=3))
        outs = ctx.enter_context(tc.tile_pool(name="outs", bufs=3))
        psum = ctx.enter_context(tc.psum_pool(name="psum", bufs=1))

        xv = x[0].rearrange("(p j) k -> p j k", j=NT)
        oqv = out_0[0].rearrange("h (p j) d -> p h j d", j=NT)
        okv = out_1[0].rearrange("(p j) d -> p j d", j=NT)
        ovv = out_2[0].rearrange("(p j) d -> p j d", j=NT)

        def bank(tag, shape):
            return psum.tile(shape, F32, name=tag)

        w_sb = consts.tile([P, 3, D], BF16, name="w_sb")
        gains = consts.tile([P, 2 * DH], BF16, name="gains")
        nc.gpsimd.memset(gains[:], 0.0)
        nc.scalar.dma_start(out=w_sb[:, 0:2, :], in_=wq.rearrange("(r p) k -> p r k", p=P))
        nc.scalar.dma_start(out=w_sb[:, 2, :], in_=wkv)
        nc.scalar.dma_start(out=gains[0:1, 0:DH], in_=q_norm_w.unsqueeze(0))
        nc.scalar.dma_start(out=gains[0:1, DH:2 * DH], in_=k_norm_w.unsqueeze(0))
        x32 = {}
        for g in range(NG):
            x_sb = xin.tile([P, GR, D], BF16, name="x_sb")
            nc.sync.dma_start(out=x_sb[:], in_=xv[:, g * GR:(g + 1) * GR, :])
            x32[g] = x_sb[:].bitcast(F32)

        ident = consts.tile([P, P], F32, name="ident")
        make_identity(nc, ident[:])
        kpi = consts.tile([P, 1], I32, name="kpi")
        nc.gpsimd.iota(kpi[:], pattern=[[0, 1]], base=0, channel_multiplier=1)
        NPOS = P + 3 * CH
        posi = consts.tile([P, NPOS], I32, name="posi")
        nc.gpsimd.iota(posi[:, 0:P], pattern=[[NT, P]], base=0, channel_multiplier=0)
        nc.gpsimd.iota(posi[:, P:P + 2 * CH], pattern=[[1, CH], [0, 2]], base=0, channel_multiplier=0)
        nc.gpsimd.iota(posi[:, P + 2 * CH:NPOS], pattern=[[CH, CH]], base=0, channel_multiplier=0)
        ones = consts.tile([P, 1], F32, name="ones")
        eps_t = consts.tile([P, 1], F32, name="eps_t")
        ones_bf = consts.tile([P, P], BF16, name="ones_bf")
        nc.vector.memset(ones[:], 1.0)
        nc.vector.memset(eps_t[:], EPS)
        nc.vector.memset(ones_bf[:], 1.0)
        warm = consts.tile([P, 2], F32, name="warm")
        nc.scalar.activation(out=warm[:, 0:1], in_=ones[:], func=ACT.Sin)
        his, los = turn_constants()
        frow = consts.tile([P, 2, NPAIR], F32, name="frow")
        for i in range(NPAIR):
            nc.vector.memset(frow[:, 0, i:i + 1], his[i])
            nc.scalar.activation(out=frow[:, 1, i:i + 1], in_=ones[:], func=ACT.Copy, scale=los[i])

        kpf = consts.tile([P, 1], F32, name="kpf")
        s4 = consts.tile([P, 1], F32, name="s4")
        php = consts.tile([P, 1], F32, name="php")
        phr = consts.tile([P, 1], F32, name="phr")
        posf = consts.tile([P, NPOS], F32, name="posf")
        mask = consts.tile([P, NPAIR], F32, name="mask")
        perm = consts.tile([P, P], F32, name="perm")
        fsel = consts.tile([P, 2, NPAIR], F32, name="fsel")
        fk = consts.tile([P, 2], F32, name="fk")
        un = consts.tile([P, NPOS], F32, name="un")
        ki = consts.tile([P, NPOS], I32, name="ki")
        NA_W = P + 2 * CH
        na = consts.tile([P, NA_W], F32, name="na")
        nb = consts.tile([P, CH], F32, name="nb")
        nb1 = consts.tile([P, CH], F32, name="nb1")
        vr = consts.tile([P, 2 * CH], F32, name="vr")
        nv = consts.tile([P, CH, P], F32, name="nv")
        nv2 = consts.tile([P, CH, P], F32, name="nv2")
        ac = consts.tile([P, CH, P], F32, name="ac")
        CC = slice(P + 2 * CH, NPOS)
        idv = ident[:].rearrange("p (i e) -> p e i", e=2)
        pmv = perm[:].rearrange("p (i e) -> p e i", e=2)
        nc.vector.tensor_copy(out=pmv[:, 0], in_=idv[:, 1])
        nc.vector.tensor_copy(out=pmv[:, 1], in_=idv[:, 0])
        nc.vector.tensor_copy(out=kpf[:], in_=kpi[:])
        nc.vector.tensor_copy(out=posf[:], in_=posi[:])
        nc.vector.tensor_scalar(out=s4[:], in0=kpf[:], scalar1=float(NPAIR), scalar2=0.25, op0=ALU.is_ge, op1=ALU.mult)
        nc.vector.tensor_tensor(out=mask[:], in0=ident[:, 0:NPAIR], in1=ident[:, NPAIR:2 * NPAIR], op=ALU.add)
        nc.vector.tensor_scalar(out=php[:], in0=s4[:], scalar1=-1.0, scalar2=0.25, op0=ALU.mult, op1=ALU.add)
        nc.vector.tensor_scalar(out=phr[:], in0=s4[:], scalar1=0.25, scalar2=None, op0=ALU.add)
        nc.vector.tensor_tensor(out=fsel[:], in0=frow[:], in1=mask[:].unsqueeze(1).to_broadcast([P, 2, NPAIR]),
                                op=ALU.mult)
        nc.vector.tensor_reduce(out=fk[:], in_=fsel[:], op=ALU.add, axis=AX.X)
        por = posf[:, P:NA_W].rearrange("p (r c) -> p c r", c=2)
        for dst in (ki, un):
            dsr = dst[:, P:NA_W].rearrange("p (r c) -> p c r", c=2)
            nc.vector.tensor_scalar(out=dst[:, CC], in0=posf[:, CC], scalar1=fk[:, 0:1], scalar2=None, op0=ALU.mult)
            for o, src, phase in ((dst[:, 0:P], posf[:, 0:P], php), (dsr[:, 0], por[:, 0], s4), (dsr[:, 1], por[:, 1], phr)):
                nc.vector.tensor_scalar(out=o, in0=src, scalar1=fk[:, 0:1], scalar2=phase[:], op0=ALU.mult, op1=ALU.add)
        nc.vector.tensor_tensor(out=un[:], in0=un[:], in1=ki[:], op=ALU.subtract)
        nc.vector.scalar_tensor_tensor(out=un[:], in0=posf[:], scalar=fk[:, 1:2], in1=un[:], op0=ALU.mult, op1=ALU.add)
        nc.vector.scalar_tensor_tensor(out=na[:], in0=un[:, 0:NA_W], scalar=0.5, in1=un[:, 0:NA_W], op0=ALU.is_ge,
                                       op1=ALU.subtract)
        nc.vector.scalar_tensor_tensor(out=nb1[:], in0=un[:, CC], scalar=0.0, in1=un[:, CC], op0=ALU.is_lt, op1=ALU.add)
        nc.vector.scalar_tensor_tensor(out=nb[:], in0=nb1[:], scalar=1.0, in1=nb1[:], op0=ALU.is_ge, op1=ALU.subtract)

        w32 = w_sb[:].bitcast(F32)
        gw = consts.tile([P, WCOLS * 4], BF16, name="gw", align_bytes=64)
        wc = consts.tile([P, WCOLS], U32, name="wc", align_bytes=64)
        ws = consts.tile([P, WCOLS], U8, name="ws", align_bytes=64)
        gwf = gw[:].bitcast(F32).rearrange("p (c u) -> p c u", u=2)
        gwb = gw[:].rearrange("p (i e u f) -> p e i u f", e=2, u=2, f=2)

        def w_transposes(dst, slot, r, mat):
            for u in range(2):
                nc.tensor.transpose(dst[:, slot + u, :], w32[:, r, u:2 * P:2], mat[:])

        def quant_w(lo, hi):
            nc.vector.quantize_mx(out=wc[:, lo:hi].bitcast(FP8X4), scales=ws[:, lo:hi], in_=gw[:, 4 * lo:4 * hi])

        pa = bank("d%d" % (ND - 1), [P, 4, P])
        w_transposes(pa, 0, 0, ident)
        w_transposes(pa, 2, 1, ident)
        pb = bank("d%d" % (ND - 2), [P, 4, P])
        w_transposes(pb, 0, 2, ident)
        nc.scalar.copy(out=gwf[:, 256:512, :].rearrange("p (r c) u -> p r c u", r=2),
                       in_=pa[:].rearrange("p (r u) c -> p r c u", u=2))
        nc.scalar.copy(out=gwf[:, 576:704, :], in_=pb[:, 0:2, :].rearrange("p u c -> p c u"))

        grp = {}
        xc_t = {}
        xs_t = {}
        base_t = {}
        tab_t = {}
        qtab_t = {}
        ps_t = {}
        ss_t = {}
        rs_t = {}
        ov_t = {}
        oq_t = {}
        ok_t = {}
        tq_t = {}
        tk_t = {}
        pq_t = {}
        pk_t = {}
        xt_t = {}
        kr_t = {}
        turn = {"a": 0, "d": 0, "x": 0}
        depth = {"a": NA, "d": ND, "x": NX}

        def next_bank(ring, shape):
            t = bank("%s%d" % (ring, turn[ring] % depth[ring]), shape)
            turn[ring] += 1
            return t

        def transposes(g, b):
            xt = next_bank("x" if NX else "a", [P, 4, P])
            xt_t[2 * g + b] = xt
            for a in range(2):
                for u in range(2):
                    nc.tensor.transpose(xt[:, 2 * a + u, :], x32[g][:, 2 * b + a, u:2 * P:2], ident[:])

        def evac(g, b, on_vector=False):
            if b == 0:
                grp[g] = grps.tile([P, GR * D], BF16, name="grp", align_bytes=64)
            grf = grp[g][:].bitcast(F32).rearrange("p (b a r u) -> p b a r u", b=2, a=2, u=2)
            src = xt_t[2 * g + b][:].rearrange("p (a u) r -> p a r u", u=2)
            if on_vector:
                nc.vector.tensor_copy(out=grf[:, b], in_=src)
            else:
                nc.scalar.copy(out=grf[:, b], in_=src)

        def quant(g):
            xc_t[g] = codes.tile([P, GR * P], U32, name="xc", align_bytes=64)
            xs_t[g] = codes.tile([P, GR * P], U8, name="xs", align_bytes=64)
            nc.vector.quantize_mx(out=xc_t[g][:].bitcast(FP8X4), scales=xs_t[g][:], in_=grp[g][:])

        brow = consts.tile([P, CH * 2 * NPAIR], F32, name="brow")

        def flat(t, lo, hi):
            return t[:, lo:hi, :].rearrange("p c n -> p (c n)")

        def angle_sums(lo, hi):
            for c in range(lo, hi):
                nc.scalar.activation(out=nv[:, c, :], in_=na[:, 0:P], func=ACT.Identity, bias=nb[:, c:c + 1])

        def wraps(lo, hi):
            nc.vector.scalar_tensor_tensor(out=flat(nv2, lo, hi), in0=flat(nv, lo, hi), scalar=-0.5,
                                           in1=flat(nv, lo, hi), op0=ALU.is_lt, op1=ALU.add)

        def sines(lo, hi):
            nc.scalar.activation(out=flat(ac, lo, hi), in_=flat(nv2, lo, hi), func=ACT.Sin, scale=-TWO_PI)

        def table(c):
            tb = next_bank("d", [P, CH, 2 * NPAIR])
            tab_t[c] = tb
            nc.tensor.matmul(out=tb[:].rearrange("p j m -> p (j m)"), lhsT=ac[:, c, :], rhs=brow[:], start=True, stop=True)

        def qgain(g, src, eng):
            half = slice(GR * (g % 2), GR * (g % 2) + GR)
            qtab_t[g] = tabs.tile([P, GR, 2 * DH], F32, name="qtab")
            eng.tensor_tensor(
                out=qtab_t[g][:].rearrange("p j (m e) -> p j m e", e=2),
                in0=src[:, half, :].unsqueeze(3).to_broadcast([P, GR, 2 * NPAIR, 2]),
                in1=gg[:].rearrange("p (m e) -> p m e", e=2).unsqueeze(1).to_broadcast([P, GR, 2 * NPAIR, 2]),
                op=ALU.mult)

        def lhs_of(j):
            g, i = divmod(j, GR)
            cols = slice(i * P, (i + 1) * P)
            return xc_t[g][:, cols].bitcast(FP8X4), xs_t[g][:, cols]

        def m1(j):
            ps = next_bank("a", [P, 384])
            ps_t[j] = ps
            lhs, lsc = lhs_of(j)
            nc.tensor.matmul_mx(out=ps[:, 0:256], lhsT=lhs, lhsT_scale=lsc, rhs=wc[:, 256:512].bitcast(FP8X4),
                                rhs_scale=ws[:, 256:512], start=True, stop=True)
            nc.tensor.matmul_mx(out=ps[:, 256:384], lhsT=lhs, lhsT_scale=lsc, rhs=wc[:, 576:704].bitcast(FP8X4),
                                rhs_scale=ws[:, 576:704], start=True, stop=True)

        def roots(g, lo, hi):
            if lo == 0:
                rs_t[g] = small.tile([P, 5 * GR], F32, name="rs")
            cols = slice(5 * lo, 5 * hi)
            nc.scalar.activation(out=rs_t[g][:, cols], in_=ss_t[g][:, cols], func=ACT.Abs_reciprocal_sqrt,
                                 scale=1.0 / DH, bias=eps_t[:])

        def squares(j):
            g, i = divmod(j, GR)
            c, jj = divmod(j, CH)
            if i == 0:
                ss_t[g] = small.tile([P, 5 * GR], F32, name="ss")
            if jj == 0:
                ov_t[c] = outs.tile([P, CH, DH], F32, name="ov")
            ps = ps_t[j]
            junk = junks.tile([P, 5, DH], BF16, name="junk")
            for h in range(5):
                nc.scalar.activation(out=junk[:, h, :], in_=ps[:, h * DH:(h + 1) * DH], func=ACT.Square,
                                     accum_out=ss_t[g][:, i * 5 + h:i * 5 + h + 1])
            nc.scalar.copy(out=ov_t[c][:, jj, :], in_=ps[:, 320:384])
            if j == GR - 1:
                roots(0, 2, GR)
            elif i == RSI and g > 1:
                roots(g - 1, 0, GR)
            elif j == NT - 1:
                roots(g, 0, GR)
            if j >= GR and i == KRI:
                k_factors(g - 1)
            if j == NT - 1:
                k_factors(g)
            if jj == CH - 1:
                nc.sync.dma_start(out=ovv[:, c * CH:(c + 1) * CH, :], in_=ov_t[c][:])

        def m2q(j):
            pq = next_bank("d", [P, 512])
            pq_t[j] = pq
            lhs, lsc = lhs_of(j)
            nc.tensor.matmul_mx(out=pq[:], lhsT=lhs, lhsT_scale=lsc, rhs=wc[:, 0:512].bitcast(FP8X4),
                                rhs_scale=ws[:, 0:512], start=True, stop=True)

        def m2k(g):
            pk = next_bank("d", [P, GR, 2 * DH])
            pk_t[g] = pk
            for i in range(GR):
                lhs, lsc = lhs_of(g * GR + i)
                nc.tensor.matmul_mx(out=pk[:, i, :], lhsT=lhs, lhsT_scale=lsc, rhs=wc[:, 512:640].bitcast(FP8X4),
                                    rhs_scale=ws[:, 512:640], start=True, stop=True)

        def rope_k(g):
            c, half = divmod(g, 2)
            tk_t[g] = work.tile([P, GR, 2 * DH], F32, name="tk")
            nc.vector.tensor_tensor(
                out=tk_t[g][:].rearrange("p j (m e) -> p (j m) e", e=2),
                in0=pk_t[g][:].rearrange("p j (m e) -> p (j m) e", e=2),
                in1=base_t[c][:, half * GR:half * GR + GR, :].rearrange("p j m -> p (j m)").unsqueeze(2).to_broadcast(
                    [P, GR * 2 * NPAIR, 2]), op=ALU.mult)

        def k_factors(g):
            kr_t[g] = work.tile([P, GR, DH], F32, name="kr")
            for i in range(GR):
                nc.scalar.activation(out=kr_t[g][:, i, :], in_=gk[:], func=ACT.Copy,
                                     scale=rs_t[g][:, i * 5 + 4:i * 5 + 5])

        def rope_q(j, first=0, last=4):
            g, i = divmod(j, GR)
            if i == 0:
                tq_t[g] = work.tile([P, GR, 512], F32, name="tq")
            pv = pq_t[j][:].rearrange("p (c h d) -> p h c d", c=2, h=4)
            tv = tq_t[g][:, i, :].rearrange("p (c h d) -> p h c d", c=2, h=4)
            for h in range(first, last):
                nc.vector.scalar_tensor_tensor(out=tv[:, h], in0=pv[:, h], scalar=rs_t[g][:, i * 5 + h:i * 5 + h + 1],
                                               in1=qtab_t[g][:, i, :].rearrange("p (c d) -> p c d", c=2), op0=ALU.mult,
                                               op1=ALU.mult)

        def add_q(eng, g, lo, hi):
            c, half = divmod(g, 2)
            if half == 0 and lo == 0:
                oq_t[c] = outs.tile([P, 4, CH, DH], F32, name="oq")
            tq = tq_t[g]
            eng.tensor_tensor(
                out=oq_t[c][:, :, half * GR + lo:half * GR + hi, :].rearrange("p h j d -> p j h d"),
                in0=tq[:, lo:hi, 0:256].rearrange("p j (h d) -> p j h d", h=4),
                in1=tq[:, lo:hi, 256:512].rearrange("p j (h d) -> p j h d", h=4), op=ALU.add)

        def add_k(g):
            c, half = divmod(g, 2)
            if half == 0:
                ok_t[c] = outs.tile([P, CH, DH], F32, name="ok")
            uk = work.tile([P, GR, DH], F32, name="uk")
            nc.gpsimd.tensor_tensor(out=uk[:], in0=tk_t[g][:, :, 0:DH], in1=tk_t[g][:, :, DH:2 * DH], op=ALU.add)
            nc.gpsimd.tensor_tensor(out=ok_t[c][:, half * GR:half * GR + GR, :], in0=uk[:],
                                    in1=kr_t[g][:], op=ALU.mult)

        def store_q(c, lo, hi):
            js = slice(c * CH + lo, c * CH + hi)
            nc.sync.dma_start(out=oqv[:, :, js, :], in_=oq_t[c][:, :, lo:hi, :])

        def store_k(c):
            nc.sync.dma_start(out=okv[:, c * CH:(c + 1) * CH, :], in_=ok_t[c][:])

        d_items = [("t", 0)]
        a_items = [("x", 0), ("x", 1), ("a", 0), ("a", 1), ("x", 2), ("x", 3), ("a", 2), ("a", 3), ("x", 4), ("a", 4),
                   ("x", 5), ("a", 5), ("x", 6), ("x", 7)]
        a_head = len(a_items)
        a_at = {}
        d_at = {}
        for v in range(NT):
            n0, m0 = len(a_items), len(d_items)
            if v + LS < NT:
                a_items.append(("a", v + LS))
            xg, xr = divmod(v + XO, GR)
            if xg < NG:
                if XR[0] == XR[1]:
                    if xr == XR[0]:
                        a_items.append(("xx", xg))
                else:
                    for half in range(2):
                        if xr == XR[half]:
                            a_items.append(("x", 2 * xg + half))
            if v % GR == 0:
                d_items.append(("k", v // GR))
            d_items.append(("q", v))
            if v % CH == TABV and v // CH + 1 < NCH:
                d_items.append(("t", v // CH + 1))
            a_at[v] = (n0, len(a_items))
            d_at[v] = (m0, len(d_items))
        made = {"a": 0, "d": 0}

        def make(ring, upto):
            items = a_items if ring == "a" else d_items
            while made[ring] < min(upto, len(items)):
                kind, n = items[made[ring]]
                made[ring] += 1
                if kind == "a":
                    m1(n)
                elif kind == "x":
                    transposes(n // 2, n % 2)
                elif kind == "xx":
                    transposes(n, 0)
                    transposes(n, 1)
                elif kind == "k":
                    m2k(n)
                elif kind == "q":
                    m2q(n)
                else:
                    table(n)

        def consume(item):
            kind, n = item
            if kind == "a":
                squares(n)
            elif kind == "x":
                evac(n // 2, n % 2)
            elif kind == "xx":
                evac(n, 0)
                evac(n, 1)
            elif kind == "k":
                rope_k(n)
            elif kind == "q":
                if n % GR == QI and n // GR + 3 < NG:
                    rope_q(n, 0, 3)
                    quant(n // GR + 3)
                    rope_q(n, 3, 4)
                else:
                    rope_q(n)
            else:
                if BASE_V or n == 0:
                    copy_base(n)
                qgain(2 * n, tab_t[n], nc.vector)
                qgain(2 * n + 1, tab_t[n], nc.vector)

        def copy_base(c):
            base_t[c] = tabs.tile([P, CH, 2 * NPAIR], F32, name="base")
            if BASE_V or c == 0:
                nc.vector.tensor_copy(out=base_t[c][:], in_=tab_t[c][:])
            else:
                nc.scalar.copy(out=base_t[c][:], in_=tab_t[c][:])

        make("a", 2)
        w_transposes(pb, 2, 2, perm)
        pc = bank("d%d" % (ND - 3), [P, 4, P])
        w_transposes(pc, 0, 0, perm)
        w_transposes(pc, 2, 1, perm)
        consume(a_items[0])
        consume(a_items[1])
        nc.scalar.activation(out=vr[:], in_=na[:, P:NA_W], func=ACT.Sin, scale=-TWO_PI)
        angle_sums(0, NCH)
        quant_w(256, 512)
        quant_w(576, 704)
        quant(0)
        make("a", 5)
        wraps(0, 1)
        sines(0, 1)
        nc.vector.tensor_tensor(out=brow[:].rearrange("p (m i) -> p m i", i=NPAIR),
                                in0=vr[:].unsqueeze(2).to_broadcast([P, 2 * CH, NPAIR]),
                                in1=mask[:].unsqueeze(1).to_broadcast([P, 2 * CH, NPAIR]), op=ALU.mult)
        wraps(1, NCH)
        nc.scalar.copy(out=gwf[:, 0:256, :].rearrange("p (r c) u -> p r c u", r=2),
                       in_=pc[:].rearrange("p (r u) c -> p r c u", u=2))
        pbv = pb[:, 2:4, 0:DH].rearrange("p u (i e) -> p e i u", e=2)
        gkv = gwf[:, 512:576, :].rearrange("p (i e) u -> p e i u", e=2)
        nc.vector.tensor_copy(out=gkv[:, 1], in_=pbv[:, 1])
        pbb = pb[:].bitcast(BF16)[:, 2:4, 0:2 * DH].rearrange("p u (i e f) -> p e i u f", e=2, f=2)
        nc.vector.tensor_scalar(out=gwb[:, 0, 256:288], in0=pbb[:, 0], scalar1=-1.0, scalar2=None, op0=ALU.mult)
        consume(a_items[2])
        consume(a_items[3])
        sines(1, NCH)
        nc.scalar.activation(out=warm[:, 1:2], in_=ones[:], func=ACT.Abs_reciprocal_sqrt)
        roots(0, 0, 2)
        pg = bank("d%d" % (ND - 2), [P, 2 * DH])
        nc.tensor.matmul(out=pg[:], lhsT=ones_bf[:], rhs=gains[:], start=True, stop=True)
        make("d", 1)
        make("a", 6)
        gg = consts.tile([P, 2 * DH], F32, name="gg")
        gk = consts.tile([P, DH], F32, name="gk")
        nc.vector.tensor_copy(out=gg[:, DH:2 * DH], in_=pg[:, 0:DH])
        ggs = gg[:, 0:DH].rearrange("p (i e) -> p e i", e=2)
        pgs = pg[:, 0:DH].rearrange("p (i e) -> p e i", e=2)
        nc.vector.tensor_scalar(out=ggs[:, 0], in0=pgs[:, 0], scalar1=-1.0, scalar2=None, op0=ALU.mult)
        nc.vector.tensor_copy(out=ggs[:, 1], in_=pgs[:, 1])
        nc.vector.tensor_copy(out=gk[:], in_=pg[:, DH:2 * DH])
        quant_w(0, 256)
        quant_w(512, 576)
        evac(1, 0, on_vector=True)
        make("a", 8)
        make("d", 4)
        evac(1, 1, on_vector=True)
        consume(a_items[6])
        consume(a_items[7])
        quant(1)
        make("a", 11)
        consume(d_items[0])
        make("d", PD + 1)
        for n in range(8, a_head):
            make("a", n + PA)
            consume(a_items[n])
        make("a", a_head + PA)

        for v in range(NT):
            g, i = divmod(v, GR)
            c, half = divmod(g, 2)
            for n in range(*d_at[v]):
                consume(d_items[n])
                make("d", n + 1 + PD)
            for n in range(*a_at[v]):
                consume(a_items[n])
            if v % CH == BASEV and v // CH + 1 < NCH and not BASE_V:
                copy_base(v // CH + 1)
            if v == 1:
                quant(2)
            make("a", a_at[v][1] + (PA if v > 0 else PA - 1))
            if i == 0:
                add_k(g)
                if half == 1:
                    store_k(c)
            if g < NG - 1:
                if i == GR - 1:
                    add_q(nc.vector if g in VECTOR_ADDS else nc.gpsimd, g, 0, GR)
                    if half == 1:
                        store_q(c, 0, CH)
            elif i == TS - 1:
                add_q(nc.gpsimd, g, 0, TS)
                store_q(c, 0, GR + TS)
            elif i == 3:
                add_q(nc.vector, g, TS, GR)
                store_q(c, GR + TS, CH)
